import numpy as np
import ml_dtypes


def mxq(x, axis, fmt="e4m3"):
    dtype, down = {"e4m3": (ml_dtypes.float8_e4m3fn, 7), "e5m2": (ml_dtypes.float8_e5m2, 14)}[fmt]
    v = np.moveaxis(np.asarray(x, np.float32).astype(ml_dtypes.bfloat16).astype(np.float64), axis, -1)
    blocks = v.reshape(v.shape[:-1] + (-1, 32))
    amax = np.abs(blocks).max(-1, keepdims=True)
    byte = np.maximum(np.where(amax > 0, np.frexp(amax)[1] - 1 + 127, 0) - down, 1)
    scale = np.exp2(byte - 127.0)
    codes = (blocks / scale).astype(np.float32).astype(dtype).astype(np.float64)
    return np.moveaxis((codes * scale).reshape(v.shape), -1, axis)


WIDE = False


def mx_kscale(k):
    if not WIDE:
        return np.ones(k)
    levels = np.array([10, -10, 5, -5, 0])
    a = np.random.permutation(np.resize(levels, k // 512 * 4)).reshape(k // 512, 4)
    idx = np.arange(k)
    return np.exp2(a[idx // 512, idx % 128 // 32])


BF16 = ml_dtypes.bfloat16


def bf(x):
    return np.asarray(x, np.float32).astype(BF16)


def f64(x):
    return np.asarray(x).astype(np.float64)


E2M1 = np.array([0.0, 0.5, 1.0, 1.5, 2.0, 3.0, 4.0, 6.0, -0.0, -0.5, -1.0, -1.5, -2.0, -3.0, -4.0, -6.0])


def pack_weight(w, fmt):
    k, n = w.shape
    w = f64(bf(w)).reshape(k // 32, 32, n)
    amax = np.abs(w).max(1)
    if fmt == "e4m3":
        byte = np.frexp(amax)[1] - 1 + 127 - 7
    else:
        mant, ex = np.frexp(amax / 6.0)
        byte = np.where(mant > 0.5, ex, ex - 1) + 127
    byte = np.clip(np.where(amax > 0, byte, 1), 1, 254)
    scaled = (w * np.exp2(127.0 - byte)[:, None, :]).reshape(k, n).astype(np.float32)
    by_word = np.ascontiguousarray(scaled.reshape(k // 512, 128, 4, n).transpose(0, 1, 3, 2))
    if fmt == "e4m3":
        words = by_word.astype(ml_dtypes.float8_e4m3fn).view(np.uint8)
    else:
        c = by_word.astype(ml_dtypes.float4_e2m1fn).view(np.uint8) & 0xF
        words = c[..., 0::2] | (c[..., 1::2] << 4)
    return np.ascontiguousarray(words), np.ascontiguousarray(byte.astype(np.uint8).reshape(k // 512, 16, n))


def unpack_weight(words, scales, fmt):
    g, p, n, _ = words.shape
    if fmt == "e4m3":
        vals = np.ascontiguousarray(words).view(ml_dtypes.float8_e4m3fn).astype(np.float64)
    else:
        nib = np.empty((g, p, n, 4), np.uint8)
        nib[..., 0::2] = words & 0xF
        nib[..., 1::2] = words >> 4
        vals = E2M1[nib]
    vals = vals * np.repeat(np.exp2(scales.astype(np.float64) - 127.0), 8, axis=1)[..., None]
    return vals.transpose(0, 1, 3, 2).reshape(g * 512, n)


S, B, ND, NS, HN, BT, C, Hd, Wd = 8, 64, 32, 96, 512, 512, 3, 64, 64
P = C * Hd * Wd
EPS = 1e-9
SELU_ALPHA = 1.6732632423543772848170429916717
SELU_SCALE = 1.0507009873554804934193349852946


def selu(v):
    return SELU_SCALE * np.where(v > 0, v, SELU_ALPHA * np.expm1(np.minimum(v, 0.0)))


def sigmoid(v):
    return 1.0 / (1.0 + np.exp(-v))


def setup_inputs():
    t = mx_kscale(HN)
    digits = bf(np.random.random_sample((S, B, ND)))
    styles = bf(np.random.standard_normal((S, B, NS)))
    images = bf(np.random.random_sample((S, B, C, Hd, Wd)))
    W_h = bf(np.random.standard_normal((ND + NS, HN)) / np.sqrt(ND + NS) * t)
    b_h = bf(np.random.standard_normal(HN) * 0.5 * t)
    W1_words, W1_scales = pack_weight(np.random.standard_normal((HN, BT)) * 1.4 / np.sqrt(HN) / t[:, None], "e4m3")
    b1 = bf(np.random.standard_normal(BT) * 0.5)
    W2_words, W2_scales = pack_weight(np.random.standard_normal((BT, P)) / np.sqrt(BT), "e4m3")
    b2 = bf(np.random.standard_normal(P) * 0.5)
    return {"digits": digits,
            "styles": styles,
            "images": images,
            "W_h": W_h,
            "b_h": b_h,
            "W1_words": W1_words,
            "W1_scales": W1_scales,
            "b1": b1,
            "W2_words": W2_words,
            "W2_scales": W2_scales,
            "b2": b2}


def reference(digits, styles, images, W_h, b_h, W1_words, W1_scales, b1, W2_words, W2_scales, b2):
    h = np.maximum(np.concatenate([f64(digits), f64(styles)], axis=-1) @ f64(W_h) + f64(b_h), 0.0)
    t = selu((mxq(h, 2, "e4m3") @ unpack_weight(W1_words, W1_scales, "e4m3")) + f64(b1))
    x_hat = sigmoid((mxq(t, 2, "e4m3") @ unpack_weight(W2_words, W2_scales, "e4m3")) + f64(b2))
    images_mean = x_hat.reshape(x_hat.shape[0], x_hat.shape[1], C, Hd, Wd)
    img = f64(images)
    loss = -(np.log(images_mean + EPS) * img + np.log(1.0 - images_mean + EPS) * (1.0 - img)).sum(-1)
    return loss

@@ -1,0 +1,297 @@
+from contextlib import ExitStack
+
+import concourse.mybir as mybir
+from concourse.masks import make_identity
+
+F32 = mybir.dt.float32
+BF16 = mybir.dt.bfloat16
+U8 = mybir.dt.uint8
+U32 = mybir.dt.uint32
+I32 = mybir.dt.int32
+FP8X4 = mybir.dt.float8_e4m3fn_x4
+ALU = mybir.AluOpType
+FUNC = mybir.ActivationFunctionType
+
+P = 128
+PACK = 4
+TOKENS = 512
+TOKEN_TILES = TOKENS // P
+HIDDEN = 512
+FEATURES = 12288
+ROW = 64
+OUTPUTS = FEATURES // ROW
+TILES = FEATURES // P
+BATCH = 32
+CHUNK = 8
+RING = BATCH // CHUNK
+Z_BANKS = 2
+WINDOW = 16
+LAG = 4
+
+EPS = 1e-9
+SELU_ALPHA = 1.6732632423543772848170429916717
+SELU_SCALE = 1.0507009873554804934193349852946
+
+FLOPS = 2 * TOKENS * (P * HIDDEN + HIDDEN * HIDDEN + HIDDEN * FEATURES)
+
+
+def tile_decoder_kernel(
+    tc, digits, styles, images, W_h, b_h, W1_words, W1_scales, b1, W2_words, W2_scales, b2, out
+):
+    nc = tc.nc
+
+    digits_v = digits.rearrange("s b d -> (s b) d").rearrange("(m p) d -> p m d", p=P)
+    styles_v = styles.rearrange("s b d -> (s b) d").rearrange("(m p) d -> p m d", p=P)
+    images_v = images.rearrange("s b c h w -> (s b) (c h w)").rearrange("(m p) f -> p m f", p=P)
+    out_v = out.rearrange("s b c h -> (s b) (c h)").rearrange("(m p) g -> p m g", p=P)
+    w1_bytes = W1_words[0].rearrange("p n t -> p (n t)")
+    w2_bytes = W2_words[0].rearrange("p n t -> p (n t)")
+
+    with ExitStack() as stack:
+        stack.enter_context(tc.manual_schedule())
+        keep = stack.enter_context(tc.tile_pool(name="keep", bufs=1))
+        x_pool = stack.enter_context(tc.tile_pool(name="x_pool", bufs=BATCH))
+        y_pool = stack.enter_context(tc.tile_pool(name="y_pool", bufs=BATCH))
+        words_pool = stack.enter_context(tc.tile_pool(name="words_pool", bufs=RING))
+        image_pool = stack.enter_context(tc.tile_pool(name="image_pool", bufs=RING))
+        psum_z = stack.enter_context(tc.psum_pool(name="psum_z", bufs=Z_BANKS))
+        psum_t = stack.enter_context(tc.psum_pool(name="psum_t", bufs=2))
+
+        cat = keep.tile([P, TOKEN_TILES, P], BF16)
+        cat_t = keep.tile([P, TOKENS], BF16)
+        wh = keep.tile([P, HIDDEN], BF16)
+        bh_rows = keep.tile([P, HIDDEN], BF16)
+        b1_rows = keep.tile([P, HIDDEN], BF16)
+        b2_rows = keep.tile([P, P], BF16)
+        b1_all = keep.tile([P, HIDDEN], F32)
+        b2_t = keep.tile([P, P], F32)
+        w1_words = keep.tile([P, HIDDEN * PACK], U8, align_bytes=64)
+        w1_plane = keep.tile([P, HIDDEN], U8, align_bytes=64)
+        w2_plane = keep.tile([P, FEATURES], U8, align_bytes=64)
+        h_grouped = keep.tile([P, TOKEN_TILES, P, PACK], BF16, align_bytes=64)
+        h_words = keep.tile([P, TOKEN_TILES, P], U32, align_bytes=64)
+        h_plane = keep.tile([P, TOKEN_TILES, P], U8, align_bytes=64)
+        t_grouped = keep.tile([P, TOKEN_TILES, P, PACK], BF16, align_bytes=64)
+        t_words = keep.tile([P, TOKENS], U32, align_bytes=64)
+        t_plane = keep.tile([P, TOKENS], U8, align_bytes=64)
+        identity = keep.tile([P, P], BF16)
+        ones = keep.tile([P, P], BF16)
+        pick = keep.tile([P, WINDOW, 2 * WINDOW], F32)
+        eps = keep.tile([P, 1], F32)
+        loss = keep.tile([P, TOKEN_TILES, OUTPUTS], F32)
+
+        nc.vector.memset(bh_rows[:], 0.0)
+        nc.vector.memset(b1_rows[:], 0.0)
+        nc.vector.memset(b2_rows[:], 0.0)
+        nc.vector.memset(w1_plane[:].bitcast(I32), 0)
+        nc.vector.memset(w2_plane[:].bitcast(I32), 0)
+        make_identity(nc, identity[:])
+        nc.gpsimd.memset(ones[:], 1.0)
+        nc.gpsimd.memset(eps[:], EPS)
+        pick_flat = pick[:].rearrange("f r c -> f (r c)")
+        pick_size = WINDOW * 2 * WINDOW
+        nc.gpsimd.memset(pick_flat, 0.0)
+        nc.gpsimd.memset(pick_flat[0:ROW, 0 : pick_size : 2 * WINDOW + 2], 1.0)
+        nc.gpsimd.memset(pick_flat[ROW:P, 1 : pick_size : 2 * WINDOW + 2], 1.0)
+
+        nc.sync.dma_start(out=cat[:, :, 0:32], in_=digits_v)
+        nc.sync.dma_start(out=cat[:, :, 32:P], in_=styles_v)
+        nc.sync.dma_start(out=wh[:], in_=W_h)
+        nc.sync.dma_start(out=w1_words[:].bitcast(I32), in_=w1_bytes.bitcast(I32))
+        nc.sync.dma_start(out=bh_rows[0:1, :], in_=b_h.rearrange("(o n) -> o n", o=1))
+        nc.sync.dma_start(out=b1_rows[0:1, :], in_=b1.rearrange("(o n) -> o n", o=1))
+        nc.sync.dma_start(out=b2_rows[0:TILES, :], in_=b2.rearrange("(i f) -> i f", f=P))
+        for quadrant in range(4):
+            rows = slice(4 * quadrant, 4 * quadrant + 4)
+            live = slice(32 * quadrant, 32 * quadrant + 4)
+            nc.sync.dma_start(out=w1_plane[live, :].bitcast(I32), in_=W1_scales[0, rows, :].bitcast(I32))
+        for quadrant in range(4):
+            rows = slice(4 * quadrant, 4 * quadrant + 4)
+            live = slice(32 * quadrant, 32 * quadrant + 4)
+            nc.sync.dma_start(out=w2_plane[live, :].bitcast(I32), in_=W2_scales[0, rows, :].bitcast(I32))
+
+        w2_chunks = {}
+        image_chunks = {}
+
+        def load_words(c):
+            chunk_bytes = CHUNK * P * PACK
+            words = words_pool.tile([P, chunk_bytes], U8, align_bytes=64)
+            source = w2_bytes[:, c * chunk_bytes : (c + 1) * chunk_bytes]
+            nc.sync.dma_start(out=words[:].bitcast(I32), in_=source.bitcast(I32))
+            w2_chunks[c] = words
+
+        def load_image(c):
+            img = image_pool.tile([P, TOKEN_TILES, CHUNK * P], BF16)
+            nc.sync.dma_start(out=img[:], in_=images_v[:, :, c * CHUNK * P : (c + 1) * CHUNK * P])
+            image_chunks[c] = img
+
+        for c in range(RING):
+            load_words(c)
+        for c in range(RING):
+            load_image(c)
+
+        cat_ps = psum_t.tile([P, TOKENS], BF16, tag="transposed")
+        for m in range(TOKEN_TILES):
+            nc.tensor.transpose(cat_ps[:, m * P : (m + 1) * P], cat[:, m, :], identity[:])
+        nc.vector.tensor_copy(out=cat_t[:], in_=cat_ps[:])
+        b1_ps = psum_z.tile([P, HIDDEN], F32, tag="z")
+        nc.tensor.matmul(out=b1_ps[:], lhsT=ones[:], rhs=b1_rows[:], start=True, stop=True)
+        nc.scalar.copy(out=b1_all[:], in_=b1_ps[:])
+        b2_ps = psum_t.tile([P, TOKENS], BF16, tag="transposed")
+        nc.tensor.transpose(b2_ps[:, 0:P], b2_rows[:], identity[:])
+        nc.vector.tensor_copy(out=b2_t[:], in_=b2_ps[:, 0:P])
+
+        wh_v = wh[:].rearrange("k (p j) -> k j p", j=PACK)
+        bh_v = bh_rows[:].rearrange("k (p j) -> k j p", j=PACK)
+
+        with tc.psum_pool(name="psum_small", bufs=2) as psum_small:
+            t_tiles = {}
+
+            def hidden_layer(m):
+                h_ps = psum_small.tile([P, PACK, P], F32, tag="h_ps")
+                for j in range(PACK):
+                    nc.tensor.matmul(
+                        out=h_ps[:, j, :], lhsT=wh_v[:, j, :], rhs=cat_t[:, m * P : (m + 1) * P],
+                        start=True, stop=False,
+                    )
+                    nc.tensor.matmul(
+                        out=h_ps[:, j, :], lhsT=bh_v[:, j, :], rhs=ones[:], start=False, stop=True
+                    )
+                nc.scalar.activation(
+                    out=h_grouped[:, m, :, :], in_=h_ps[:].rearrange("p j t -> p t j"), func=FUNC.Relu
+                )
+                nc.vector.quantize_mx(
+                    out=h_words[:, m, :].bitcast(FP8X4),
+                    scales=h_plane[:, m, :],
+                    in_=h_grouped[:, m, :, :].rearrange("p t j -> p (t j)"),
+                )
+
+            def bottleneck_layer(m):
+                t_ps = psum_small.tile([P, HIDDEN], F32, tag="t_ps")
+                nc.tensor.matmul_mx(
+                    out=t_ps[:],
+                    lhsT=h_words[:, m, :].bitcast(FP8X4),
+                    lhsT_scale=h_plane[:, m, :],
+                    rhs=w1_words[:].bitcast(FP8X4),
+                    rhs_scale=w1_plane[:],
+                    start=True,
+                    stop=True,
+                )
+                u = x_pool.tile([P, HIDDEN], F32, tag="x")
+                nc.vector.tensor_tensor(out=u[:], in0=t_ps[:], in1=b1_all[:], op=ALU.add)
+                e = y_pool.tile([P, HIDDEN], F32, tag="y")
+                nc.scalar.activation(out=e[:], in_=u[:], func=FUNC.Exp)
+                r = x_pool.tile([P, HIDDEN], F32, tag="x")
+                nc.scalar.activation(out=r[:], in_=u[:], func=FUNC.Relu, scale=SELU_SCALE)
+                nc.vector.tensor_scalar(
+                    out=e[:], in0=e[:], scalar1=1.0, scalar2=SELU_SCALE * SELU_ALPHA,
+                    op0=ALU.min, op1=ALU.mult,
+                )
+                t_sb = keep.tile([P, HIDDEN], BF16, tag="t_sb", bufs=2)
+                nc.vector.scalar_tensor_tensor(
+                    out=t_sb[:], in0=e[:], scalar=-SELU_SCALE * SELU_ALPHA, in1=r[:],
+                    op0=ALU.add, op1=ALU.add,
+                )
+                t_tiles[m] = t_sb
+
+            def regroup(m):
+                t_v = t_tiles[m][:].rearrange("t (p j) -> t j p", j=PACK)
+                t_ps_t = psum_t.tile([P, PACK, P], BF16, tag="transposed")
+                for j in range(PACK):
+                    nc.tensor.transpose(t_ps_t[:, j, :], t_v[:, j, :], identity[:])
+                nc.scalar.copy(out=t_grouped[:, m, :, :], in_=t_ps_t[:].rearrange("p j t -> p t j"))
+                nc.vector.quantize_mx(
+                    out=t_words[:, m * P : (m + 1) * P].bitcast(FP8X4),
+                    scales=t_plane[:, m * P : (m + 1) * P],
+                    in_=t_grouped[:, m, :, :].rearrange("p t j -> p (t j)"),
+                )
+
+            for step_m in range(TOKEN_TILES + 2):
+                if step_m < TOKEN_TILES:
+                    hidden_layer(step_m)
+                if 0 <= step_m - 1 < TOKEN_TILES:
+                    bottleneck_layer(step_m - 1)
+                if 0 <= step_m - 2 < TOKEN_TILES:
+                    regroup(step_m - 2)
+
+        psum_sums = stack.enter_context(tc.psum_pool(name="psum_sums", bufs=1))
+        sums = [psum_sums.tile([P, OUTPUTS], F32, name="sums%d" % m) for m in range(TOKEN_TILES)]
+        z_tiles = {}
+        x_tiles = {}
+        y_tiles = {}
+
+        def product(i):
+            c, k = divmod(i, CHUNK)
+            z = psum_z.tile([P, TOKENS], F32, tag="z")
+            nc.tensor.matmul_mx(
+                out=z[:],
+                lhsT=w2_chunks[c][:, k * P * PACK : (k + 1) * P * PACK].bitcast(FP8X4),
+                lhsT_scale=w2_plane[:, i * P : (i + 1) * P],
+                rhs=t_words[:].bitcast(FP8X4),
+                rhs_scale=t_plane[:],
+                start=True,
+                stop=True,
+            )
+            z_tiles[i] = z
+            if k == CHUNK - 1 and c + RING < TILES // CHUNK:
+                load_words(c + RING)
+
+        def sigmoid(i):
+            x = x_pool.tile([P, TOKENS], F32, tag="x")
+            nc.scalar.activation(out=x[:], in_=z_tiles[i][:], func=FUNC.Sigmoid, bias=b2_t[:, i : i + 1])
+            y = y_pool.tile([P, TOKENS], F32, tag="y")
+            nc.vector.tensor_scalar(
+                out=y[:], in0=x[:], scalar1=-1.0, scalar2=1.0, op0=ALU.mult, op1=ALU.add
+            )
+            x_tiles[i] = x
+            y_tiles[i] = y
+
+        def logs_and_products(i):
+            c, k = divmod(i, CHUNK)
+            x = x_tiles[i]
+            y = y_tiles[i]
+            nc.scalar.activation(out=x[:], in_=x[:], func=FUNC.Ln, bias=eps[:])
+            nc.scalar.activation(out=y[:], in_=y[:], func=FUNC.Ln, bias=eps[:])
+            img_t = psum_t.tile([P, TOKENS], BF16, tag="transposed")
+            for m in range(TOKEN_TILES):
+                nc.tensor.transpose(
+                    img_t[:, m * P : (m + 1) * P], image_chunks[c][:, m, k * P : (k + 1) * P], identity[:]
+                )
+            if k == CHUNK - 1 and c + RING < TILES // CHUNK:
+                load_image(c + RING)
+            nc.vector.tensor_tensor(out=x[:], in0=img_t[:], in1=x[:], op=ALU.mult)
+            nc.vector.scalar_tensor_tensor(
+                out=y[:], in0=img_t[:], scalar=1.0, in1=y[:], op0=ALU.subtract, op1=ALU.mult
+            )
+            nc.gpsimd.tensor_tensor(out=y[:], in0=y[:], in1=x[:], op=ALU.subtract)
+
+        def row_sums(i):
+            w, r = divmod(i, WINDOW)
+            for m in range(TOKEN_TILES):
+                nc.tensor.matmul(
+                    out=sums[m][:, w * 2 * WINDOW : (w + 1) * 2 * WINDOW],
+                    lhsT=y_tiles[i][:, m * P : (m + 1) * P],
+                    rhs=pick[:, r, :],
+                    start=(r == 0),
+                    stop=(r == WINDOW - 1),
+                )
+
+        for i in range(Z_BANKS):
+            product(i)
+        for first in range(0, TILES, BATCH):
+            for k in range(BATCH):
+                sigmoid(first + k)
+                if first + k + Z_BANKS < TILES:
+                    product(first + k + Z_BANKS)
+                if first > 0 and k % 2 == 1 and k // 2 < LAG:
+                    row_sums(first - LAG + k // 2)
+            for k in range(BATCH):
+                logs_and_products(first + k)
+                if k >= LAG:
+                    row_sums(first + k - LAG)
+        for i in range(TILES - LAG, TILES):
+            row_sums(i)
+
+        for m in range(TOKEN_TILES):
+            nc.vector.tensor_copy(out=loss[:, m, :], in_=sums[m][:])
+        nc.sync.dma_start(out=out_v, in_=loss[:])

@@ -25,7 +25,7 @@ BATCH = 32
 CHUNK = 8
 RING = BATCH // CHUNK
 Z_BANKS = 2
-WINDOW = 16
+WINDOW = 24
 LAG = 4
 
 EPS = 1e-9
@@ -60,10 +60,9 @@ def tile_decoder_kernel(
         cat = keep.tile([P, TOKEN_TILES, P], BF16)
         cat_t = keep.tile([P, TOKENS], BF16)
         wh = keep.tile([P, HIDDEN], BF16)
-        bh_rows = keep.tile([P, HIDDEN], BF16)
-        b1_rows = keep.tile([P, HIDDEN], BF16)
+        bh = keep.tile([P, PACK], BF16)
+        b1_all = keep.tile([P, HIDDEN], BF16)
         b2_rows = keep.tile([P, P], BF16)
-        b1_all = keep.tile([P, HIDDEN], F32)
         b2_t = keep.tile([P, P], F32)
         w1_words = keep.tile([P, HIDDEN * PACK], U8, align_bytes=64)
         w1_plane = keep.tile([P, HIDDEN], U8, align_bytes=64)
@@ -75,18 +74,14 @@ def tile_decoder_kernel(
         t_words = keep.tile([P, TOKENS], U32, align_bytes=64)
         t_plane = keep.tile([P, TOKENS], U8, align_bytes=64)
         identity = keep.tile([P, P], BF16)
-        ones = keep.tile([P, P], BF16)
         pick = keep.tile([P, WINDOW, 2 * WINDOW], F32)
         eps = keep.tile([P, 1], F32)
         loss = keep.tile([P, TOKEN_TILES, OUTPUTS], F32)
 
-        nc.vector.memset(bh_rows[:], 0.0)
-        nc.vector.memset(b1_rows[:], 0.0)
         nc.vector.memset(b2_rows[:], 0.0)
         nc.vector.memset(w1_plane[:].bitcast(I32), 0)
         nc.vector.memset(w2_plane[:].bitcast(I32), 0)
         make_identity(nc, identity[:])
-        nc.gpsimd.memset(ones[:], 1.0)
         nc.gpsimd.memset(eps[:], EPS)
         pick_flat = pick[:].rearrange("f r c -> f (r c)")
         pick_size = WINDOW * 2 * WINDOW
@@ -98,8 +93,8 @@ def tile_decoder_kernel(
         nc.sync.dma_start(out=cat[:, :, 32:P], in_=styles_v)
         nc.sync.dma_start(out=wh[:], in_=W_h)
         nc.sync.dma_start(out=w1_words[:].bitcast(I32), in_=w1_bytes.bitcast(I32))
-        nc.sync.dma_start(out=bh_rows[0:1, :], in_=b_h.rearrange("(o n) -> o n", o=1))
-        nc.sync.dma_start(out=b1_rows[0:1, :], in_=b1.rearrange("(o n) -> o n", o=1))
+        nc.sync.dma_start(out=bh[:], in_=b_h.rearrange("(p j) -> p j", j=PACK))
+        nc.sync.dma_start(out=b1_all[:], in_=b1.partition_broadcast(P))
         nc.sync.dma_start(out=b2_rows[0:TILES, :], in_=b2.rearrange("(i f) -> i f", f=P))
         for quadrant in range(4):
             rows = slice(4 * quadrant, 4 * quadrant + 4)
@@ -134,15 +129,12 @@ def tile_decoder_kernel(
         for m in range(TOKEN_TILES):
             nc.tensor.transpose(cat_ps[:, m * P : (m + 1) * P], cat[:, m, :], identity[:])
         nc.vector.tensor_copy(out=cat_t[:], in_=cat_ps[:])
-        b1_ps = psum_z.tile([P, HIDDEN], F32, tag="z")
-        nc.tensor.matmul(out=b1_ps[:], lhsT=ones[:], rhs=b1_rows[:], start=True, stop=True)
-        nc.scalar.copy(out=b1_all[:], in_=b1_ps[:])
         b2_ps = psum_t.tile([P, TOKENS], BF16, tag="transposed")
         nc.tensor.transpose(b2_ps[:, 0:P], b2_rows[:], identity[:])
         nc.vector.tensor_copy(out=b2_t[:], in_=b2_ps[:, 0:P])
 
         wh_v = wh[:].rearrange("k (p j) -> k j p", j=PACK)
-        bh_v = bh_rows[:].rearrange("k (p j) -> k j p", j=PACK)
+        bh_v = bh[:].unsqueeze(1).to_broadcast([P, P, PACK])
 
         with tc.psum_pool(name="psum_small", bufs=2) as psum_small:
             t_tiles = {}
@@ -152,14 +144,13 @@ def tile_decoder_kernel(
                 for j in range(PACK):
                     nc.tensor.matmul(
                         out=h_ps[:, j, :], lhsT=wh_v[:, j, :], rhs=cat_t[:, m * P : (m + 1) * P],
-                        start=True, stop=False,
+                        start=True, stop=True,
                     )
-                    nc.tensor.matmul(
-                        out=h_ps[:, j, :], lhsT=bh_v[:, j, :], rhs=ones[:], start=False, stop=True
-                    )
-                nc.scalar.activation(
-                    out=h_grouped[:, m, :, :], in_=h_ps[:].rearrange("p j t -> p t j"), func=FUNC.Relu
+                h_sum = x_pool.tile([P, P, PACK], F32, tag="x")
+                nc.vector.tensor_tensor(
+                    out=h_sum[:], in0=h_ps[:].rearrange("p j t -> p t j"), in1=bh_v, op=ALU.add
                 )
+                nc.scalar.activation(out=h_grouped[:, m, :, :], in_=h_sum[:], func=FUNC.Relu)
                 nc.vector.quantize_mx(
                     out=h_words[:, m, :].bitcast(FP8X4),
                     scales=h_plane[:, m, :],
@@ -265,9 +256,9 @@ def tile_decoder_kernel(
             )
             nc.gpsimd.tensor_tensor(out=y[:], in0=y[:], in1=x[:], op=ALU.subtract)
 
-        def row_sums(i):
+        def row_sums(i, token_tiles):
             w, r = divmod(i, WINDOW)
-            for m in range(TOKEN_TILES):
+            for m in token_tiles:
                 nc.tensor.matmul(
                     out=sums[m][:, w * 2 * WINDOW : (w + 1) * 2 * WINDOW],
                     lhsT=y_tiles[i][:, m * P : (m + 1) * P],
@@ -276,21 +267,27 @@ def tile_decoder_kernel(
                     stop=(r == WINDOW - 1),
                 )
 
+        early = range(TOKEN_TILES - 1)
+        late = range(TOKEN_TILES - 1, TOKEN_TILES)
         for i in range(Z_BANKS):
             product(i)
         for first in range(0, TILES, BATCH):
             for k in range(BATCH):
+                if first > 0:
+                    if k % 2 == 1 and k // 2 < LAG:
+                        row_sums(first - LAG + k // 2, early)
+                    row_sums(first - BATCH + k, late)
                 sigmoid(first + k)
                 if first + k + Z_BANKS < TILES:
                     product(first + k + Z_BANKS)
-                if first > 0 and k % 2 == 1 and k // 2 < LAG:
-                    row_sums(first - LAG + k // 2)
             for k in range(BATCH):
                 logs_and_products(first + k)
                 if k >= LAG:
-                    row_sums(first + k - LAG)
+                    row_sums(first + k - LAG, early)
         for i in range(TILES - LAG, TILES):
-            row_sums(i)
+            row_sums(i, early)
+        for i in range(TILES - BATCH, TILES):
+            row_sums(i, late)
 
         for m in range(TOKEN_TILES):
             nc.vector.tensor_copy(out=loss[:, m, :], in_=sums[m][:])

@@ -254,7 +254,7 @@ def tile_decoder_kernel(
             nc.vector.scalar_tensor_tensor(
                 out=y[:], in0=img_t[:], scalar=1.0, in1=y[:], op0=ALU.subtract, op1=ALU.mult
             )
-            nc.gpsimd.tensor_tensor(out=y[:], in0=y[:], in1=x[:], op=ALU.subtract)
+            nc.vector.tensor_tensor(out=y[:], in0=y[:], in1=x[:], op=ALU.subtract)
 
         def row_sums(i, token_tiles):
             w, r = divmod(i, WINDOW)

@@ -11,6 +11,7 @@ I32 = mybir.dt.int32
 FP8X4 = mybir.dt.float8_e4m3fn_x4
 ALU = mybir.AluOpType
 FUNC = mybir.ActivationFunctionType
+AXIS = mybir.AxisListType
 
 P = 128
 PACK = 4
@@ -20,13 +21,18 @@ HIDDEN = 512
 FEATURES = 12288
 ROW = 64
 OUTPUTS = FEATURES // ROW
-TILES = FEATURES // P
-BATCH = 32
-CHUNK = 8
-RING = BATCH // CHUNK
-Z_BANKS = 2
-WINDOW = 24
-LAG = 4
+HALVES = 2
+SLAB = HALVES * P
+SLABS = FEATURES // SLAB
+BATCH = 12
+BATCHES = SLABS // BATCH
+LIVE = 16
+CHUNK = 4
+CHUNKS = SLABS // CHUNK
+RING = 4
+SIGMOID_FROM = 7
+SIGMOID_SLABS = 3
+SIGMOID_STEPS = BATCH // SIGMOID_SLABS
 
 EPS = 1e-9
 SELU_ALPHA = 1.6732632423543772848170429916717
@@ -50,11 +56,11 @@ def tile_decoder_kernel(
     with ExitStack() as stack:
         stack.enter_context(tc.manual_schedule())
         keep = stack.enter_context(tc.tile_pool(name="keep", bufs=1))
-        x_pool = stack.enter_context(tc.tile_pool(name="x_pool", bufs=BATCH))
-        y_pool = stack.enter_context(tc.tile_pool(name="y_pool", bufs=BATCH))
+        x_pool = stack.enter_context(tc.tile_pool(name="x_pool", bufs=LIVE))
+        y_pool = stack.enter_context(tc.tile_pool(name="y_pool", bufs=LIVE))
         words_pool = stack.enter_context(tc.tile_pool(name="words_pool", bufs=RING))
         image_pool = stack.enter_context(tc.tile_pool(name="image_pool", bufs=RING))
-        psum_z = stack.enter_context(tc.psum_pool(name="psum_z", bufs=Z_BANKS))
+        psum_z = stack.enter_context(tc.psum_pool(name="psum_z", bufs=2))
         psum_t = stack.enter_context(tc.psum_pool(name="psum_t", bufs=2))
 
         cat = keep.tile([P, TOKEN_TILES, P], BF16)
@@ -74,7 +80,7 @@ def tile_decoder_kernel(
         t_words = keep.tile([P, TOKENS], U32, align_bytes=64)
         t_plane = keep.tile([P, TOKENS], U8, align_bytes=64)
         identity = keep.tile([P, P], BF16)
-        pick = keep.tile([P, WINDOW, 2 * WINDOW], F32)
+        identity_f32 = keep.tile([P, P], F32)
         eps = keep.tile([P, 1], F32)
         loss = keep.tile([P, TOKEN_TILES, OUTPUTS], F32)
 
@@ -82,12 +88,8 @@ def tile_decoder_kernel(
         nc.vector.memset(w1_plane[:].bitcast(I32), 0)
         nc.vector.memset(w2_plane[:].bitcast(I32), 0)
         make_identity(nc, identity[:])
+        make_identity(nc, identity_f32[:])
         nc.gpsimd.memset(eps[:], EPS)
-        pick_flat = pick[:].rearrange("f r c -> f (r c)")
-        pick_size = WINDOW * 2 * WINDOW
-        nc.gpsimd.memset(pick_flat, 0.0)
-        nc.gpsimd.memset(pick_flat[0:ROW, 0 : pick_size : 2 * WINDOW + 2], 1.0)
-        nc.gpsimd.memset(pick_flat[ROW:P, 1 : pick_size : 2 * WINDOW + 2], 1.0)
 
         nc.sync.dma_start(out=cat[:, :, 0:32], in_=digits_v)
         nc.sync.dma_start(out=cat[:, :, 32:P], in_=styles_v)
@@ -95,7 +97,7 @@ def tile_decoder_kernel(
         nc.sync.dma_start(out=w1_words[:].bitcast(I32), in_=w1_bytes.bitcast(I32))
         nc.sync.dma_start(out=bh[:], in_=b_h.rearrange("(p j) -> p j", j=PACK))
         nc.sync.dma_start(out=b1_all[:], in_=b1.partition_broadcast(P))
-        nc.sync.dma_start(out=b2_rows[0:TILES, :], in_=b2.rearrange("(i f) -> i f", f=P))
+        nc.sync.dma_start(out=b2_rows[0 : FEATURES // P, :], in_=b2.rearrange("(i f) -> i f", f=P))
         for quadrant in range(4):
             rows = slice(4 * quadrant, 4 * quadrant + 4)
             live = slice(32 * quadrant, 32 * quadrant + 4)
@@ -109,15 +111,15 @@ def tile_decoder_kernel(
         image_chunks = {}
 
         def load_words(c):
-            chunk_bytes = CHUNK * P * PACK
+            chunk_bytes = CHUNK * SLAB * PACK
             words = words_pool.tile([P, chunk_bytes], U8, align_bytes=64)
             source = w2_bytes[:, c * chunk_bytes : (c + 1) * chunk_bytes]
             nc.sync.dma_start(out=words[:].bitcast(I32), in_=source.bitcast(I32))
             w2_chunks[c] = words
 
         def load_image(c):
-            img = image_pool.tile([P, TOKEN_TILES, CHUNK * P], BF16)
-            nc.sync.dma_start(out=img[:], in_=images_v[:, :, c * CHUNK * P : (c + 1) * CHUNK * P])
+            img = image_pool.tile([P, TOKEN_TILES, CHUNK * SLAB], BF16)
+            nc.sync.dma_start(out=img[:], in_=images_v[:, :, c * CHUNK * SLAB : (c + 1) * CHUNK * SLAB])
             image_chunks[c] = img
 
         for c in range(RING):
@@ -197,98 +199,121 @@ def tile_decoder_kernel(
                     in_=t_grouped[:, m, :, :].rearrange("p t j -> p (t j)"),
                 )
 
-            for step_m in range(TOKEN_TILES + 2):
-                if step_m < TOKEN_TILES:
-                    hidden_layer(step_m)
-                if 0 <= step_m - 1 < TOKEN_TILES:
-                    bottleneck_layer(step_m - 1)
-                if 0 <= step_m - 2 < TOKEN_TILES:
-                    regroup(step_m - 2)
+            for step in range(TOKEN_TILES + 2):
+                if step < TOKEN_TILES:
+                    hidden_layer(step)
+                if 0 <= step - 1 < TOKEN_TILES:
+                    bottleneck_layer(step - 1)
+                if 0 <= step - 2 < TOKEN_TILES:
+                    regroup(step - 2)
 
-        psum_sums = stack.enter_context(tc.psum_pool(name="psum_sums", bufs=1))
-        sums = [psum_sums.tile([P, OUTPUTS], F32, name="sums%d" % m) for m in range(TOKEN_TILES)]
-        z_tiles = {}
+        psum_back = stack.enter_context(tc.psum_pool(name="psum_back", bufs=2 * HALVES))
         x_tiles = {}
         y_tiles = {}
+        image_t = {}
+        loss_t = {}
 
-        def product(i):
-            c, k = divmod(i, CHUNK)
-            z = psum_z.tile([P, TOKENS], F32, tag="z")
-            nc.tensor.matmul_mx(
-                out=z[:],
-                lhsT=w2_chunks[c][:, k * P * PACK : (k + 1) * P * PACK].bitcast(FP8X4),
-                lhsT_scale=w2_plane[:, i * P : (i + 1) * P],
-                rhs=t_words[:].bitcast(FP8X4),
-                rhs_scale=t_plane[:],
-                start=True,
-                stop=True,
-            )
-            z_tiles[i] = z
-            if k == CHUNK - 1 and c + RING < TILES // CHUNK:
+        def sigmoids(s):
+            c, k = divmod(s, CHUNK)
+            x = x_pool.tile([P, HALVES, TOKENS], F32, tag="x")
+            for half in range(HALVES):
+                i = HALVES * s + half
+                first_byte = (HALVES * k + half) * P * PACK
+                z = psum_z.tile([P, TOKENS], F32, tag="z")
+                nc.tensor.matmul_mx(
+                    out=z[:],
+                    lhsT=w2_chunks[c][:, first_byte : first_byte + P * PACK].bitcast(FP8X4),
+                    lhsT_scale=w2_plane[:, i * P : (i + 1) * P],
+                    rhs=t_words[:].bitcast(FP8X4),
+                    rhs_scale=t_plane[:],
+                    start=True,
+                    stop=True,
+                )
+                nc.scalar.activation(out=x[:, half, :], in_=z[:], func=FUNC.Sigmoid, bias=b2_t[:, i : i + 1])
+            x_tiles[s] = x
+            if k == CHUNK - 1 and c + RING < CHUNKS:
                 load_words(c + RING)
 
-        def sigmoid(i):
-            x = x_pool.tile([P, TOKENS], F32, tag="x")
-            nc.scalar.activation(out=x[:], in_=z_tiles[i][:], func=FUNC.Sigmoid, bias=b2_t[:, i : i + 1])
-            y = y_pool.tile([P, TOKENS], F32, tag="y")
+        def one_minus(s):
+            y = y_pool.tile([P, HALVES, TOKENS], F32, tag="y")
             nc.vector.tensor_scalar(
-                out=y[:], in0=x[:], scalar1=-1.0, scalar2=1.0, op0=ALU.mult, op1=ALU.add
+                out=y[:], in0=x_tiles[s][:], scalar1=-1.0, scalar2=1.0, op0=ALU.mult, op1=ALU.add
             )
-            x_tiles[i] = x
-            y_tiles[i] = y
+            y_tiles[s] = y
 
-        def logs_and_products(i):
-            c, k = divmod(i, CHUNK)
-            x = x_tiles[i]
-            y = y_tiles[i]
-            nc.scalar.activation(out=x[:], in_=x[:], func=FUNC.Ln, bias=eps[:])
-            nc.scalar.activation(out=y[:], in_=y[:], func=FUNC.Ln, bias=eps[:])
-            img_t = psum_t.tile([P, TOKENS], BF16, tag="transposed")
-            for m in range(TOKEN_TILES):
-                nc.tensor.transpose(
-                    img_t[:, m * P : (m + 1) * P], image_chunks[c][:, m, k * P : (k + 1) * P], identity[:]
-                )
-            if k == CHUNK - 1 and c + RING < TILES // CHUNK:
+        def logs(s):
+            nc.scalar.activation(out=x_tiles[s][:], in_=x_tiles[s][:], func=FUNC.Ln, bias=eps[:])
+            nc.scalar.activation(out=y_tiles[s][:], in_=y_tiles[s][:], func=FUNC.Ln, bias=eps[:])
+
+        def transpose_image(s):
+            c, k = divmod(s, CHUNK)
+            img_t = psum_t.tile([P, HALVES, TOKENS], BF16, tag="transposed")
+            for half in range(HALVES):
+                first = (HALVES * k + half) * P
+                for m in range(TOKEN_TILES):
+                    nc.tensor.transpose(
+                        img_t[:, half, m * P : (m + 1) * P], image_chunks[c][:, m, first : first + P], identity[:]
+                    )
+            image_t[s] = img_t
+            if k == CHUNK - 1 and c + RING < CHUNKS:
                 load_image(c + RING)
-            nc.vector.tensor_tensor(out=x[:], in0=img_t[:], in1=x[:], op=ALU.mult)
-            nc.vector.scalar_tensor_tensor(
-                out=y[:], in0=img_t[:], scalar=1.0, in1=y[:], op0=ALU.subtract, op1=ALU.mult
-            )
-            nc.vector.tensor_tensor(out=y[:], in0=y[:], in1=x[:], op=ALU.subtract)
 
-        def row_sums(i, token_tiles):
-            w, r = divmod(i, WINDOW)
-            for m in token_tiles:
-                nc.tensor.matmul(
-                    out=sums[m][:, w * 2 * WINDOW : (w + 1) * 2 * WINDOW],
-                    lhsT=y_tiles[i][:, m * P : (m + 1) * P],
-                    rhs=pick[:, r, :],
-                    start=(r == 0),
-                    stop=(r == WINDOW - 1),
+        def products(s):
+            x = x_tiles[s]
+            y = y_tiles[s]
+            nc.vector.tensor_tensor(out=x[:], in0=image_t[s][:], in1=x[:], op=ALU.mult)
+            nc.vector.scalar_tensor_tensor(
+                out=y[:], in0=image_t[s][:], scalar=1.0, in1=y[:], op0=ALU.subtract, op1=ALU.mult
+            )
+            nc.gpsimd.tensor_tensor(out=y[:], in0=y[:], in1=x[:], op=ALU.subtract)
+
+        def transpose_loss(s):
+            loss_t[s] = []
+            for half in range(HALVES):
+                back = psum_back.tile([P, TOKEN_TILES, P], F32, tag="back")
+                for m in range(TOKEN_TILES):
+                    nc.tensor.transpose(back[:, m, :], y_tiles[s][:, half, m * P : (m + 1) * P], identity_f32[:])
+                loss_t[s].append(back)
+
+        def row_sums(s):
+            for half in range(HALVES):
+                g = (HALVES * s + half) * (P // ROW)
+                nc.vector.tensor_reduce(
+                    out=loss[:, :, g : g + P // ROW],
+                    in_=loss_t[s][half][:].rearrange("p m (g w) -> p m g w", w=ROW),
+                    axis=AXIS.X,
+                    op=ALU.add,
                 )
 
-        early = range(TOKEN_TILES - 1)
-        late = range(TOKEN_TILES - 1, TOKEN_TILES)
-        for i in range(Z_BANKS):
-            product(i)
-        for first in range(0, TILES, BATCH):
+        for s in range(BATCH):
+            sigmoids(s)
+            one_minus(s)
+        transpose_image(0)
+        for batch in range(BATCHES):
             for k in range(BATCH):
-                if first > 0:
-                    if k % 2 == 1 and k // 2 < LAG:
-                        row_sums(first - LAG + k // 2, early)
-                    row_sums(first - BATCH + k, late)
-                sigmoid(first + k)
-                if first + k + Z_BANKS < TILES:
-                    product(first + k + Z_BANKS)
+                logs(batch * BATCH + k)
             for k in range(BATCH):
-                logs_and_products(first + k)
-                if k >= LAG:
-                    row_sums(first + k - LAG, early)
-        for i in range(TILES - LAG, TILES):
-            row_sums(i, early)
-        for i in range(TILES - BATCH, TILES):
-            row_sums(i, late)
-
-        for m in range(TOKEN_TILES):
-            nc.vector.tensor_copy(out=loss[:, m, :], in_=sums[m][:])
+                s = batch * BATCH + k
+                ahead = []
+                if batch + 1 < BATCHES and 0 <= k - SIGMOID_FROM < SIGMOID_STEPS:
+                    first = (batch + 1) * BATCH + (k - SIGMOID_FROM) * SIGMOID_SLABS
+                    ahead = list(range(first, first + SIGMOID_SLABS))
+                if ahead:
+                    sigmoids(ahead[0])
+                if s + 1 < SLABS:
+                    transpose_image(s + 1)
+                if ahead:
+                    sigmoids(ahead[1])
+                if s >= 1:
+                    transpose_loss(s - 1)
+                if ahead:
+                    sigmoids(ahead[2])
+                products(s)
+                if s >= 2:
+                    row_sums(s - 2)
+                for a in ahead:
+                    one_minus(a)
+        transpose_loss(SLABS - 1)
+        row_sums(SLABS - 2)
+        row_sums(SLABS - 1)
         nc.sync.dma_start(out=out_v, in_=loss[:])

@@ -24,14 +24,14 @@ OUTPUTS = FEATURES // ROW
 HALVES = 2
 SLAB = HALVES * P
 SLABS = FEATURES // SLAB
-BATCH = 12
+BATCH = 8
 BATCHES = SLABS // BATCH
-LIVE = 16
+LIVE = 12
 CHUNK = 4
 CHUNKS = SLABS // CHUNK
 RING = 4
-SIGMOID_FROM = 7
-SIGMOID_SLABS = 3
+SIGMOID_FROM = 5
+SIGMOID_SLABS = 4
 SIGMOID_STEPS = BATCH // SIGMOID_SLABS
 
 EPS = 1e-9
@@ -66,7 +66,7 @@ def tile_decoder_kernel(
         cat = keep.tile([P, TOKEN_TILES, P], BF16)
         cat_t = keep.tile([P, TOKENS], BF16)
         wh = keep.tile([P, HIDDEN], BF16)
-        bh = keep.tile([P, PACK], BF16)
+        bh_rows = keep.tile([P, HIDDEN], BF16)
         b1_all = keep.tile([P, HIDDEN], BF16)
         b2_rows = keep.tile([P, P], BF16)
         b2_t = keep.tile([P, P], F32)
@@ -81,21 +81,24 @@ def tile_decoder_kernel(
         t_plane = keep.tile([P, TOKENS], U8, align_bytes=64)
         identity = keep.tile([P, P], BF16)
         identity_f32 = keep.tile([P, P], F32)
+        ones = keep.tile([P, P], BF16)
         eps = keep.tile([P, 1], F32)
         loss = keep.tile([P, TOKEN_TILES, OUTPUTS], F32)
 
+        nc.vector.memset(bh_rows[:], 0.0)
         nc.vector.memset(b2_rows[:], 0.0)
         nc.vector.memset(w1_plane[:].bitcast(I32), 0)
         nc.vector.memset(w2_plane[:].bitcast(I32), 0)
         make_identity(nc, identity[:])
         make_identity(nc, identity_f32[:])
+        nc.gpsimd.memset(ones[:], 1.0)
         nc.gpsimd.memset(eps[:], EPS)
 
         nc.sync.dma_start(out=cat[:, :, 0:32], in_=digits_v)
         nc.sync.dma_start(out=cat[:, :, 32:P], in_=styles_v)
         nc.sync.dma_start(out=wh[:], in_=W_h)
         nc.sync.dma_start(out=w1_words[:].bitcast(I32), in_=w1_bytes.bitcast(I32))
-        nc.sync.dma_start(out=bh[:], in_=b_h.rearrange("(p j) -> p j", j=PACK))
+        nc.sync.dma_start(out=bh_rows[0:1, :], in_=b_h.rearrange("(o n) -> o n", o=1))
         nc.sync.dma_start(out=b1_all[:], in_=b1.partition_broadcast(P))
         nc.sync.dma_start(out=b2_rows[0 : FEATURES // P, :], in_=b2.rearrange("(i f) -> i f", f=P))
         for quadrant in range(4):
@@ -136,33 +139,42 @@ def tile_decoder_kernel(
         nc.vector.tensor_copy(out=b2_t[:], in_=b2_ps[:, 0:P])
 
         wh_v = wh[:].rearrange("k (p j) -> k j p", j=PACK)
-        bh_v = bh[:].unsqueeze(1).to_broadcast([P, P, PACK])
+        bh_v = bh_rows[:].rearrange("k (p j) -> k j p", j=PACK)
 
         with tc.psum_pool(name="psum_small", bufs=2) as psum_small:
-            t_tiles = {}
+            h_ps = {}
+            t_ps = {}
+            u = {}
+            e = {}
+            r = {}
+            t_sb = {}
+            t_ps_t = {}
 
-            def hidden_layer(m):
-                h_ps = psum_small.tile([P, PACK, P], F32, tag="h_ps")
+            def hidden_matmuls(m):
+                h_ps[m] = psum_small.tile([P, PACK, P], F32, tag="h_ps", name="h_ps")
                 for j in range(PACK):
                     nc.tensor.matmul(
-                        out=h_ps[:, j, :], lhsT=wh_v[:, j, :], rhs=cat_t[:, m * P : (m + 1) * P],
-                        start=True, stop=True,
+                        out=h_ps[m][:, j, :], lhsT=wh_v[:, j, :], rhs=cat_t[:, m * P : (m + 1) * P],
+                        start=True, stop=False,
                     )
-                h_sum = x_pool.tile([P, P, PACK], F32, tag="x")
-                nc.vector.tensor_tensor(
-                    out=h_sum[:], in0=h_ps[:].rearrange("p j t -> p t j"), in1=bh_v, op=ALU.add
+                    nc.tensor.matmul(
+                        out=h_ps[m][:, j, :], lhsT=bh_v[:, j, :], rhs=ones[:], start=False, stop=True
+                    )
+
+            def relu(m):
+                nc.scalar.activation(
+                    out=h_grouped[:, m, :, :], in_=h_ps[m][:].rearrange("p j t -> p t j"), func=FUNC.Relu
                 )
-                nc.scalar.activation(out=h_grouped[:, m, :, :], in_=h_sum[:], func=FUNC.Relu)
+
+            def bottleneck_matmul(m):
                 nc.vector.quantize_mx(
                     out=h_words[:, m, :].bitcast(FP8X4),
                     scales=h_plane[:, m, :],
                     in_=h_grouped[:, m, :, :].rearrange("p t j -> p (t j)"),
                 )
-
-            def bottleneck_layer(m):
-                t_ps = psum_small.tile([P, HIDDEN], F32, tag="t_ps")
+                t_ps[m] = psum_small.tile([P, HIDDEN], F32, tag="t_ps", name="t_ps")
                 nc.tensor.matmul_mx(
-                    out=t_ps[:],
+                    out=t_ps[m][:],
                     lhsT=h_words[:, m, :].bitcast(FP8X4),
                     lhsT_scale=h_plane[:, m, :],
                     rhs=w1_words[:].bitcast(FP8X4),
@@ -170,42 +182,50 @@ def tile_decoder_kernel(
                     start=True,
                     stop=True,
                 )
-                u = x_pool.tile([P, HIDDEN], F32, tag="x")
-                nc.vector.tensor_tensor(out=u[:], in0=t_ps[:], in1=b1_all[:], op=ALU.add)
-                e = y_pool.tile([P, HIDDEN], F32, tag="y")
-                nc.scalar.activation(out=e[:], in_=u[:], func=FUNC.Exp)
-                r = x_pool.tile([P, HIDDEN], F32, tag="x")
-                nc.scalar.activation(out=r[:], in_=u[:], func=FUNC.Relu, scale=SELU_SCALE)
+
+            def add_b1(m):
+                u[m] = x_pool.tile([P, HIDDEN], F32, tag="x", name="u")
+                nc.vector.tensor_tensor(out=u[m][:], in0=t_ps[m][:], in1=b1_all[:], op=ALU.add)
+
+            def selu_on_scalar(m):
+                e[m] = y_pool.tile([P, HIDDEN], F32, tag="y", name="e")
+                nc.scalar.activation(out=e[m][:], in_=u[m][:], func=FUNC.Exp)
+                r[m] = x_pool.tile([P, HIDDEN], F32, tag="x", name="r")
+                nc.scalar.activation(out=r[m][:], in_=u[m][:], func=FUNC.Relu, scale=SELU_SCALE)
+
+            def selu_on_vector(m):
                 nc.vector.tensor_scalar(
-                    out=e[:], in0=e[:], scalar1=1.0, scalar2=SELU_SCALE * SELU_ALPHA,
+                    out=e[m][:], in0=e[m][:], scalar1=1.0, scalar2=SELU_SCALE * SELU_ALPHA,
                     op0=ALU.min, op1=ALU.mult,
                 )
-                t_sb = keep.tile([P, HIDDEN], BF16, tag="t_sb", bufs=2)
+                t_sb[m] = keep.tile([P, HIDDEN], BF16, tag="t_sb", bufs=2, name="t_sb")
                 nc.vector.scalar_tensor_tensor(
-                    out=t_sb[:], in0=e[:], scalar=-SELU_SCALE * SELU_ALPHA, in1=r[:],
+                    out=t_sb[m][:], in0=e[m][:], scalar=-SELU_SCALE * SELU_ALPHA, in1=r[m][:],
                     op0=ALU.add, op1=ALU.add,
                 )
-                t_tiles[m] = t_sb
-
-            def regroup(m):
-                t_v = t_tiles[m][:].rearrange("t (p j) -> t j p", j=PACK)
-                t_ps_t = psum_t.tile([P, PACK, P], BF16, tag="transposed")
+                t_v = t_sb[m][:].rearrange("t (p j) -> t j p", j=PACK)
+                t_ps_t[m] = psum_t.tile([P, PACK, P], BF16, tag="transposed", name="t_ps_t")
                 for j in range(PACK):
-                    nc.tensor.transpose(t_ps_t[:, j, :], t_v[:, j, :], identity[:])
-                nc.scalar.copy(out=t_grouped[:, m, :, :], in_=t_ps_t[:].rearrange("p j t -> p t j"))
+                    nc.tensor.transpose(t_ps_t[m][:, j, :], t_v[:, j, :], identity[:])
+
+            def group_t(m):
+                nc.scalar.copy(out=t_grouped[:, m, :, :], in_=t_ps_t[m][:].rearrange("p j t -> p t j"))
+
+            def quantise_t(m):
                 nc.vector.quantize_mx(
                     out=t_words[:, m * P : (m + 1) * P].bitcast(FP8X4),
                     scales=t_plane[:, m * P : (m + 1) * P],
                     in_=t_grouped[:, m, :, :].rearrange("p t j -> p (t j)"),
                 )
 
-            for step in range(TOKEN_TILES + 2):
-                if step < TOKEN_TILES:
-                    hidden_layer(step)
-                if 0 <= step - 1 < TOKEN_TILES:
-                    bottleneck_layer(step - 1)
-                if 0 <= step - 2 < TOKEN_TILES:
-                    regroup(step - 2)
+            stages = [
+                hidden_matmuls, relu, bottleneck_matmul, add_b1,
+                selu_on_scalar, selu_on_vector, group_t, quantise_t,
+            ]
+            for tick in range(TOKEN_TILES + len(stages) - 1):
+                for depth in reversed(range(len(stages))):
+                    if 0 <= tick - depth < TOKEN_TILES:
+                        stages[depth](tick - depth)
 
         psum_back = stack.enter_context(tc.psum_pool(name="psum_back", bufs=2 * HALVES))
         x_tiles = {}
@@ -237,7 +257,10 @@ def tile_decoder_kernel(
         def one_minus(s):
             y = y_pool.tile([P, HALVES, TOKENS], F32, tag="y")
             nc.vector.tensor_scalar(
-                out=y[:], in0=x_tiles[s][:], scalar1=-1.0, scalar2=1.0, op0=ALU.mult, op1=ALU.add
+                out=y[:, 0, :], in0=x_tiles[s][:, 0, :], scalar1=-1.0, scalar2=1.0, op0=ALU.mult, op1=ALU.add
+            )
+            nc.gpsimd.tensor_scalar(
+                out=y[:, 1, :], in0=x_tiles[s][:, 1, :], scalar1=-1.0, scalar2=1.0, op0=ALU.mult, op1=ALU.add
             )
             y_tiles[s] = y
 
@@ -284,36 +307,39 @@ def tile_decoder_kernel(
                     axis=AXIS.X,
                     op=ALU.add,
                 )
+            if (s + 1) % BATCH == 0:
+                done = slice((s + 1 - BATCH) * SLAB // ROW, (s + 1) * SLAB // ROW)
+                nc.sync.dma_start(out=out_v[:, :, done], in_=loss[:, :, done])
 
         for s in range(BATCH):
             sigmoids(s)
             one_minus(s)
         transpose_image(0)
+        def slabs_ahead(batch, k):
+            if batch + 1 < BATCHES and 0 <= k - SIGMOID_FROM < SIGMOID_STEPS:
+                first = (batch + 1) * BATCH + (k - SIGMOID_FROM) * SIGMOID_SLABS
+                return list(range(first, first + SIGMOID_SLABS))
+            return []
+
         for batch in range(BATCHES):
             for k in range(BATCH):
                 logs(batch * BATCH + k)
             for k in range(BATCH):
                 s = batch * BATCH + k
-                ahead = []
-                if batch + 1 < BATCHES and 0 <= k - SIGMOID_FROM < SIGMOID_STEPS:
-                    first = (batch + 1) * BATCH + (k - SIGMOID_FROM) * SIGMOID_SLABS
-                    ahead = list(range(first, first + SIGMOID_SLABS))
-                if ahead:
-                    sigmoids(ahead[0])
+                ahead = slabs_ahead(batch, k)
+                for a in ahead[:1]:
+                    sigmoids(a)
                 if s + 1 < SLABS:
                     transpose_image(s + 1)
-                if ahead:
-                    sigmoids(ahead[1])
+                for a in ahead[1:]:
+                    sigmoids(a)
                 if s >= 1:
                     transpose_loss(s - 1)
-                if ahead:
-                    sigmoids(ahead[2])
                 products(s)
                 if s >= 2:
                     row_sums(s - 2)
-                for a in ahead:
+                for a in slabs_ahead(batch, k - 1):
                     one_minus(a)
         transpose_loss(SLABS - 1)
         row_sums(SLABS - 2)
         row_sums(SLABS - 1)
-        nc.sync.dma_start(out=out_v, in_=loss[:])

@@ -30,7 +30,8 @@ LIVE = 12
 CHUNK = 4
 CHUNKS = SLABS // CHUNK
 RING = 4
-SIGMOID_FROM = 5
+Z_BANKS = 4
+SIGMOID_FROM = 4
 SIGMOID_SLABS = 4
 SIGMOID_STEPS = BATCH // SIGMOID_SLABS
 
@@ -60,8 +61,9 @@ def tile_decoder_kernel(
         y_pool = stack.enter_context(tc.tile_pool(name="y_pool", bufs=LIVE))
         words_pool = stack.enter_context(tc.tile_pool(name="words_pool", bufs=RING))
         image_pool = stack.enter_context(tc.tile_pool(name="image_pool", bufs=RING))
-        psum_z = stack.enter_context(tc.psum_pool(name="psum_z", bufs=2))
+        psum_z = stack.enter_context(tc.psum_pool(name="psum_z", bufs=Z_BANKS))
         psum_t = stack.enter_context(tc.psum_pool(name="psum_t", bufs=2))
+        psum_back = stack.enter_context(tc.psum_pool(name="psum_back", bufs=HALVES))
 
         cat = keep.tile([P, TOKEN_TILES, P], BF16)
         cat_t = keep.tile([P, TOKENS], BF16)
@@ -141,93 +143,91 @@ def tile_decoder_kernel(
         wh_v = wh[:].rearrange("k (p j) -> k j p", j=PACK)
         bh_v = bh_rows[:].rearrange("k (p j) -> k j p", j=PACK)
 
-        with tc.psum_pool(name="psum_small", bufs=2) as psum_small:
-            h_ps = {}
-            t_ps = {}
-            u = {}
-            e = {}
-            r = {}
-            t_sb = {}
-            t_ps_t = {}
+        h_ps = {}
+        t_ps = {}
+        u = {}
+        e = {}
+        r = {}
+        t_sb = {}
+        t_ps_t = {}
 
-            def hidden_matmuls(m):
-                h_ps[m] = psum_small.tile([P, PACK, P], F32, tag="h_ps", name="h_ps")
-                for j in range(PACK):
-                    nc.tensor.matmul(
-                        out=h_ps[m][:, j, :], lhsT=wh_v[:, j, :], rhs=cat_t[:, m * P : (m + 1) * P],
-                        start=True, stop=False,
-                    )
-                    nc.tensor.matmul(
-                        out=h_ps[m][:, j, :], lhsT=bh_v[:, j, :], rhs=ones[:], start=False, stop=True
-                    )
-
-            def relu(m):
-                nc.scalar.activation(
-                    out=h_grouped[:, m, :, :], in_=h_ps[m][:].rearrange("p j t -> p t j"), func=FUNC.Relu
+        def hidden_matmuls(m):
+            h_ps[m] = psum_z.tile([P, PACK, P], F32, tag="z", name="h_ps")
+            for j in range(PACK):
+                nc.tensor.matmul(
+                    out=h_ps[m][:, j, :], lhsT=wh_v[:, j, :], rhs=cat_t[:, m * P : (m + 1) * P],
+                    start=True, stop=False,
+                )
+                nc.tensor.matmul(
+                    out=h_ps[m][:, j, :], lhsT=bh_v[:, j, :], rhs=ones[:], start=False, stop=True
                 )
 
-            def bottleneck_matmul(m):
-                nc.vector.quantize_mx(
-                    out=h_words[:, m, :].bitcast(FP8X4),
-                    scales=h_plane[:, m, :],
-                    in_=h_grouped[:, m, :, :].rearrange("p t j -> p (t j)"),
-                )
-                t_ps[m] = psum_small.tile([P, HIDDEN], F32, tag="t_ps", name="t_ps")
-                nc.tensor.matmul_mx(
-                    out=t_ps[m][:],
-                    lhsT=h_words[:, m, :].bitcast(FP8X4),
-                    lhsT_scale=h_plane[:, m, :],
-                    rhs=w1_words[:].bitcast(FP8X4),
-                    rhs_scale=w1_plane[:],
-                    start=True,
-                    stop=True,
-                )
+        def relu(m):
+            nc.scalar.activation(
+                out=h_grouped[:, m, :, :], in_=h_ps[m][:].rearrange("p j t -> p t j"), func=FUNC.Relu
+            )
 
-            def add_b1(m):
-                u[m] = x_pool.tile([P, HIDDEN], F32, tag="x", name="u")
-                nc.vector.tensor_tensor(out=u[m][:], in0=t_ps[m][:], in1=b1_all[:], op=ALU.add)
+        def bottleneck_matmul(m):
+            nc.vector.quantize_mx(
+                out=h_words[:, m, :].bitcast(FP8X4),
+                scales=h_plane[:, m, :],
+                in_=h_grouped[:, m, :, :].rearrange("p t j -> p (t j)"),
+            )
+            t_ps[m] = psum_z.tile([P, HIDDEN], F32, tag="z", name="t_ps")
+            nc.tensor.matmul_mx(
+                out=t_ps[m][:],
+                lhsT=h_words[:, m, :].bitcast(FP8X4),
+                lhsT_scale=h_plane[:, m, :],
+                rhs=w1_words[:].bitcast(FP8X4),
+                rhs_scale=w1_plane[:],
+                start=True,
+                stop=True,
+            )
 
-            def selu_on_scalar(m):
-                e[m] = y_pool.tile([P, HIDDEN], F32, tag="y", name="e")
-                nc.scalar.activation(out=e[m][:], in_=u[m][:], func=FUNC.Exp)
-                r[m] = x_pool.tile([P, HIDDEN], F32, tag="x", name="r")
-                nc.scalar.activation(out=r[m][:], in_=u[m][:], func=FUNC.Relu, scale=SELU_SCALE)
+        def add_b1(m):
+            u[m] = x_pool.tile([P, HIDDEN], F32, tag="x", name="u")
+            nc.vector.tensor_tensor(out=u[m][:], in0=t_ps[m][:], in1=b1_all[:], op=ALU.add)
 
-            def selu_on_vector(m):
-                nc.vector.tensor_scalar(
-                    out=e[m][:], in0=e[m][:], scalar1=1.0, scalar2=SELU_SCALE * SELU_ALPHA,
-                    op0=ALU.min, op1=ALU.mult,
-                )
-                t_sb[m] = keep.tile([P, HIDDEN], BF16, tag="t_sb", bufs=2, name="t_sb")
-                nc.vector.scalar_tensor_tensor(
-                    out=t_sb[m][:], in0=e[m][:], scalar=-SELU_SCALE * SELU_ALPHA, in1=r[m][:],
-                    op0=ALU.add, op1=ALU.add,
-                )
-                t_v = t_sb[m][:].rearrange("t (p j) -> t j p", j=PACK)
-                t_ps_t[m] = psum_t.tile([P, PACK, P], BF16, tag="transposed", name="t_ps_t")
-                for j in range(PACK):
-                    nc.tensor.transpose(t_ps_t[m][:, j, :], t_v[:, j, :], identity[:])
+        def selu_on_scalar(m):
+            e[m] = y_pool.tile([P, HIDDEN], F32, tag="y", name="e")
+            nc.scalar.activation(out=e[m][:], in_=u[m][:], func=FUNC.Exp)
+            r[m] = x_pool.tile([P, HIDDEN], F32, tag="x", name="r")
+            nc.scalar.activation(out=r[m][:], in_=u[m][:], func=FUNC.Relu, scale=SELU_SCALE)
 
-            def group_t(m):
-                nc.scalar.copy(out=t_grouped[:, m, :, :], in_=t_ps_t[m][:].rearrange("p j t -> p t j"))
+        def selu_on_vector(m):
+            nc.vector.tensor_scalar(
+                out=e[m][:], in0=e[m][:], scalar1=1.0, scalar2=SELU_SCALE * SELU_ALPHA,
+                op0=ALU.min, op1=ALU.mult,
+            )
+            t_sb[m] = keep.tile([P, HIDDEN], BF16, tag="t_sb", bufs=2, name="t_sb")
+            nc.vector.scalar_tensor_tensor(
+                out=t_sb[m][:], in0=e[m][:], scalar=-SELU_SCALE * SELU_ALPHA, in1=r[m][:],
+                op0=ALU.add, op1=ALU.add,
+            )
+            t_v = t_sb[m][:].rearrange("t (p j) -> t j p", j=PACK)
+            t_ps_t[m] = psum_t.tile([P, PACK, P], BF16, tag="transposed", name="t_ps_t")
+            for j in range(PACK):
+                nc.tensor.transpose(t_ps_t[m][:, j, :], t_v[:, j, :], identity[:])
 
-            def quantise_t(m):
-                nc.vector.quantize_mx(
-                    out=t_words[:, m * P : (m + 1) * P].bitcast(FP8X4),
-                    scales=t_plane[:, m * P : (m + 1) * P],
-                    in_=t_grouped[:, m, :, :].rearrange("p t j -> p (t j)"),
-                )
+        def group_t(m):
+            nc.scalar.copy(out=t_grouped[:, m, :, :], in_=t_ps_t[m][:].rearrange("p j t -> p t j"))
 
-            stages = [
-                hidden_matmuls, relu, bottleneck_matmul, add_b1,
-                selu_on_scalar, selu_on_vector, group_t, quantise_t,
-            ]
-            for tick in range(TOKEN_TILES + len(stages) - 1):
-                for depth in reversed(range(len(stages))):
-                    if 0 <= tick - depth < TOKEN_TILES:
-                        stages[depth](tick - depth)
+        def quantise_t(m):
+            nc.vector.quantize_mx(
+                out=t_words[:, m * P : (m + 1) * P].bitcast(FP8X4),
+                scales=t_plane[:, m * P : (m + 1) * P],
+                in_=t_grouped[:, m, :, :].rearrange("p t j -> p (t j)"),
+            )
 
-        psum_back = stack.enter_context(tc.psum_pool(name="psum_back", bufs=2 * HALVES))
+        stages = [
+            hidden_matmuls, relu, bottleneck_matmul, add_b1,
+            selu_on_scalar, selu_on_vector, group_t, quantise_t,
+        ]
+        for tick in range(TOKEN_TILES + len(stages) - 1):
+            for depth in reversed(range(len(stages))):
+                if 0 <= tick - depth < TOKEN_TILES:
+                    stages[depth](tick - depth)
+
         x_tiles = {}
         y_tiles = {}
         image_t = {}
@@ -333,13 +333,13 @@ def tile_decoder_kernel(
                     transpose_image(s + 1)
                 for a in ahead[1:]:
                     sigmoids(a)
-                if s >= 1:
-                    transpose_loss(s - 1)
                 products(s)
-                if s >= 2:
-                    row_sums(s - 2)
                 for a in slabs_ahead(batch, k - 1):
                     one_minus(a)
-        transpose_loss(SLABS - 1)
+                if s >= 2:
+                    row_sums(s - 2)
+                if s >= 1:
+                    transpose_loss(s - 1)
         row_sums(SLABS - 2)
+        transpose_loss(SLABS - 1)
         row_sums(SLABS - 1)

@@ -1,4 +1,5 @@
 from contextlib import ExitStack
+import math
 
 import concourse.mybir as mybir
 from concourse.masks import make_identity
@@ -24,18 +25,21 @@ OUTPUTS = FEATURES // ROW
 HALVES = 2
 SLAB = HALVES * P
 SLABS = FEATURES // SLAB
-BATCH = 8
-BATCHES = SLABS // BATCH
-LIVE = 12
+BATCHES = (6, 12, 14, 11, 5)
+LIVE = 17
 CHUNK = 4
 CHUNKS = SLABS // CHUNK
-RING = 4
+RAW_RING = 3
+WORDS_RING = 3
+IMAGE_RING = 4
 Z_BANKS = 4
-SIGMOID_FROM = 4
-SIGMOID_SLABS = 4
-SIGMOID_STEPS = BATCH // SIGMOID_SLABS
+Z_LEAD = Z_BANKS // HALVES
 
 EPS = 1e-9
+D = EPS / (1.0 + EPS)
+ODDS = 1.0 / D - D
+A_SCALE = ODDS / (1.0 + 2.0 * EPS)
+A_SHIFT = (1.0 + D) / ODDS
 SELU_ALPHA = 1.6732632423543772848170429916717
 SELU_SCALE = 1.0507009873554804934193349852946
 
@@ -59,22 +63,24 @@ def tile_decoder_kernel(
         keep = stack.enter_context(tc.tile_pool(name="keep", bufs=1))
         x_pool = stack.enter_context(tc.tile_pool(name="x_pool", bufs=LIVE))
         y_pool = stack.enter_context(tc.tile_pool(name="y_pool", bufs=LIVE))
-        words_pool = stack.enter_context(tc.tile_pool(name="words_pool", bufs=RING))
-        image_pool = stack.enter_context(tc.tile_pool(name="image_pool", bufs=RING))
+        raw_pool = stack.enter_context(tc.tile_pool(name="raw_pool", bufs=RAW_RING))
+        words_pool = stack.enter_context(tc.tile_pool(name="words_pool", bufs=WORDS_RING))
+        image_pool = stack.enter_context(tc.tile_pool(name="image_pool", bufs=IMAGE_RING))
         psum_z = stack.enter_context(tc.psum_pool(name="psum_z", bufs=Z_BANKS))
         psum_t = stack.enter_context(tc.psum_pool(name="psum_t", bufs=2))
-        psum_back = stack.enter_context(tc.psum_pool(name="psum_back", bufs=HALVES))
+        psum_back = stack.enter_context(tc.psum_pool(name="psum_back", bufs=2))
 
         cat = keep.tile([P, TOKEN_TILES, P], BF16)
         cat_t = keep.tile([P, TOKENS], BF16)
         wh = keep.tile([P, HIDDEN], BF16)
         bh_rows = keep.tile([P, HIDDEN], BF16)
         b1_all = keep.tile([P, HIDDEN], BF16)
-        b2_rows = keep.tile([P, P], BF16)
-        b2_t = keep.tile([P, P], F32)
+        b2_rows = keep.tile([P, SLAB], BF16)
+        b2_t = keep.tile([P, HALVES, P], F32)
         w1_words = keep.tile([P, HIDDEN * PACK], U8, align_bytes=64)
         w1_plane = keep.tile([P, HIDDEN], U8, align_bytes=64)
-        w2_plane = keep.tile([P, FEATURES], U8, align_bytes=64)
+        w2_raw_plane = keep.tile([P, FEATURES], U8, align_bytes=64)
+        w2_plane = keep.tile([P, SLABS, HALVES, P], U8, align_bytes=64)
         h_grouped = keep.tile([P, TOKEN_TILES, P, PACK], BF16, align_bytes=64)
         h_words = keep.tile([P, TOKEN_TILES, P], U32, align_bytes=64)
         h_plane = keep.tile([P, TOKEN_TILES, P], U8, align_bytes=64)
@@ -84,17 +90,15 @@ def tile_decoder_kernel(
         identity = keep.tile([P, P], BF16)
         identity_f32 = keep.tile([P, P], F32)
         ones = keep.tile([P, P], BF16)
-        eps = keep.tile([P, 1], F32)
         loss = keep.tile([P, TOKEN_TILES, OUTPUTS], F32)
 
         nc.vector.memset(bh_rows[:], 0.0)
         nc.vector.memset(b2_rows[:], 0.0)
         nc.vector.memset(w1_plane[:].bitcast(I32), 0)
-        nc.vector.memset(w2_plane[:].bitcast(I32), 0)
+        nc.vector.memset(w2_raw_plane[:].bitcast(I32), 0)
         make_identity(nc, identity[:])
         make_identity(nc, identity_f32[:])
         nc.gpsimd.memset(ones[:], 1.0)
-        nc.gpsimd.memset(eps[:], EPS)
 
         nc.sync.dma_start(out=cat[:, :, 0:32], in_=digits_v)
         nc.sync.dma_start(out=cat[:, :, 32:P], in_=styles_v)
@@ -102,7 +106,7 @@ def tile_decoder_kernel(
         nc.sync.dma_start(out=w1_words[:].bitcast(I32), in_=w1_bytes.bitcast(I32))
         nc.sync.dma_start(out=bh_rows[0:1, :], in_=b_h.rearrange("(o n) -> o n", o=1))
         nc.sync.dma_start(out=b1_all[:], in_=b1.partition_broadcast(P))
-        nc.sync.dma_start(out=b2_rows[0 : FEATURES // P, :], in_=b2.rearrange("(i f) -> i f", f=P))
+        nc.sync.dma_start(out=b2_rows[0:SLABS, :], in_=b2.rearrange("(s f) -> s f", f=SLAB))
         for quadrant in range(4):
             rows = slice(4 * quadrant, 4 * quadrant + 4)
             live = slice(32 * quadrant, 32 * quadrant + 4)
@@ -110,35 +114,50 @@ def tile_decoder_kernel(
         for quadrant in range(4):
             rows = slice(4 * quadrant, 4 * quadrant + 4)
             live = slice(32 * quadrant, 32 * quadrant + 4)
-            nc.sync.dma_start(out=w2_plane[live, :].bitcast(I32), in_=W2_scales[0, rows, :].bitcast(I32))
+            nc.sync.dma_start(out=w2_raw_plane[live, :].bitcast(I32), in_=W2_scales[0, rows, :].bitcast(I32))
 
+        raw_chunks = {}
         w2_chunks = {}
         image_chunks = {}
 
         def load_words(c):
-            chunk_bytes = CHUNK * SLAB * PACK
-            words = words_pool.tile([P, chunk_bytes], U8, align_bytes=64)
-            source = w2_bytes[:, c * chunk_bytes : (c + 1) * chunk_bytes]
-            nc.sync.dma_start(out=words[:].bitcast(I32), in_=source.bitcast(I32))
-            w2_chunks[c] = words
+            width = CHUNK * SLAB
+            raw = raw_pool.tile([P, width], I32)
+            nc.sync.dma_start(out=raw[:], in_=w2_bytes.bitcast(I32)[:, c * width : (c + 1) * width])
+            raw_chunks[c] = raw
 
         def load_image(c):
             img = image_pool.tile([P, TOKEN_TILES, CHUNK * SLAB], BF16)
             nc.sync.dma_start(out=img[:], in_=images_v[:, :, c * CHUNK * SLAB : (c + 1) * CHUNK * SLAB])
             image_chunks[c] = img
 
-        for c in range(RING):
+        def split_words(c):
+            words = words_pool.tile([P, CHUNK, HALVES, P], U32, align_bytes=64)
+            nc.vector.tensor_copy(
+                out=words[:].bitcast(I32), in_=raw_chunks[c][:].rearrange("p (s i j) -> p s j i", j=HALVES, i=P)
+            )
+            slabs = slice(c * CHUNK, (c + 1) * CHUNK)
+            nc.gpsimd.tensor_copy(
+                out=w2_plane[:, slabs, :, :],
+                in_=w2_raw_plane[:].rearrange("p (s i j) -> p s j i", j=HALVES, i=P)[:, slabs, :, :],
+            )
+            w2_chunks[c] = words
+            if c + RAW_RING < CHUNKS:
+                load_words(c + RAW_RING)
+
+        for c in range(RAW_RING):
             load_words(c)
-        for c in range(RING):
+        for c in range(IMAGE_RING):
             load_image(c)
 
         cat_ps = psum_t.tile([P, TOKENS], BF16, tag="transposed")
         for m in range(TOKEN_TILES):
             nc.tensor.transpose(cat_ps[:, m * P : (m + 1) * P], cat[:, m, :], identity[:])
         nc.vector.tensor_copy(out=cat_t[:], in_=cat_ps[:])
-        b2_ps = psum_t.tile([P, TOKENS], BF16, tag="transposed")
-        nc.tensor.transpose(b2_ps[:, 0:P], b2_rows[:], identity[:])
-        nc.vector.tensor_copy(out=b2_t[:], in_=b2_ps[:, 0:P])
+        b2_ps = psum_t.tile([P, HALVES, P], BF16, tag="transposed")
+        for j in range(HALVES):
+            nc.tensor.transpose(b2_ps[:, j, :], b2_rows[:, j::HALVES], identity[:])
+        nc.vector.tensor_scalar_add(b2_t[:], b2_ps[:], math.log(D))
 
         wh_v = wh[:].rearrange("k (p j) -> k j p", j=PACK)
         bh_v = bh_rows[:].rearrange("k (p j) -> k j p", j=PACK)
@@ -223,123 +242,143 @@ def tile_decoder_kernel(
             hidden_matmuls, relu, bottleneck_matmul, add_b1,
             selu_on_scalar, selu_on_vector, group_t, quantise_t,
         ]
+        split_words(0)
         for tick in range(TOKEN_TILES + len(stages) - 1):
             for depth in reversed(range(len(stages))):
                 if 0 <= tick - depth < TOKEN_TILES:
                     stages[depth](tick - depth)
 
+        z_tiles = {}
         x_tiles = {}
         y_tiles = {}
         image_t = {}
         loss_t = {}
 
-        def sigmoids(s):
+        def products_z(s):
             c, k = divmod(s, CHUNK)
-            x = x_pool.tile([P, HALVES, TOKENS], F32, tag="x")
+            if k == 0 and c + 1 < CHUNKS:
+                split_words(c + 1)
             for half in range(HALVES):
-                i = HALVES * s + half
-                first_byte = (HALVES * k + half) * P * PACK
                 z = psum_z.tile([P, TOKENS], F32, tag="z")
                 nc.tensor.matmul_mx(
                     out=z[:],
-                    lhsT=w2_chunks[c][:, first_byte : first_byte + P * PACK].bitcast(FP8X4),
-                    lhsT_scale=w2_plane[:, i * P : (i + 1) * P],
+                    lhsT=w2_chunks[c][:, k, half, :].bitcast(FP8X4),
+                    lhsT_scale=w2_plane[:, s, half, :],
                     rhs=t_words[:].bitcast(FP8X4),
                     rhs_scale=t_plane[:],
                     start=True,
                     stop=True,
                 )
-                nc.scalar.activation(out=x[:, half, :], in_=z[:], func=FUNC.Sigmoid, bias=b2_t[:, i : i + 1])
-            x_tiles[s] = x
-            if k == CHUNK - 1 and c + RING < CHUNKS:
-                load_words(c + RING)
+                z_tiles[s, half] = z
 
-        def one_minus(s):
-            y = y_pool.tile([P, HALVES, TOKENS], F32, tag="y")
-            nc.vector.tensor_scalar(
-                out=y[:, 0, :], in0=x_tiles[s][:, 0, :], scalar1=-1.0, scalar2=1.0, op0=ALU.mult, op1=ALU.add
-            )
+        def sigmoids(s):
+            x = x_pool.tile([P, HALVES, TOKENS], F32, tag="x")
+            for half in range(HALVES):
+                nc.scalar.activation(
+                    out=x[:, half, :], in_=z_tiles[s, half][:], func=FUNC.Sigmoid, bias=b2_t[:, half, s : s + 1]
+                )
+            x_tiles[s] = x
+            if s + Z_LEAD < SLABS:
+                products_z(s + Z_LEAD)
+            y = y_pool.tile([P, TOKENS], F32, tag="y")
             nc.gpsimd.tensor_scalar(
-                out=y[:, 1, :], in0=x_tiles[s][:, 1, :], scalar1=-1.0, scalar2=1.0, op0=ALU.mult, op1=ALU.add
+                out=y[:], in0=x[:, 1, :], scalar1=1.0, scalar2=A_SHIFT, op0=ALU.mult, op1=ALU.add
             )
             y_tiles[s] = y
 
+        def pair(s):
+            y = y_tiles[s]
+            nc.vector.scalar_tensor_tensor(
+                out=y[:], in0=x_tiles[s][:, 0, :], scalar=A_SHIFT, in1=y[:], op0=ALU.add, op1=ALU.mult
+            )
+
         def logs(s):
-            nc.scalar.activation(out=x_tiles[s][:], in_=x_tiles[s][:], func=FUNC.Ln, bias=eps[:])
-            nc.scalar.activation(out=y_tiles[s][:], in_=y_tiles[s][:], func=FUNC.Ln, bias=eps[:])
+            x = x_tiles[s]
+            y = y_tiles[s]
+            nc.scalar.activation(out=x[:], in_=x[:], func=FUNC.Ln, scale=ODDS, bias=D)
+            nc.scalar.activation(out=y[:], in_=y[:], func=FUNC.Ln, scale=A_SCALE * A_SCALE)
 
         def transpose_image(s):
             c, k = divmod(s, CHUNK)
             img_t = psum_t.tile([P, HALVES, TOKENS], BF16, tag="transposed")
             for half in range(HALVES):
-                first = (HALVES * k + half) * P
                 for m in range(TOKEN_TILES):
                     nc.tensor.transpose(
-                        img_t[:, half, m * P : (m + 1) * P], image_chunks[c][:, m, first : first + P], identity[:]
+                        img_t[:, half, m * P : (m + 1) * P],
+                        image_chunks[c][:, m, k * SLAB + half : (k + 1) * SLAB : HALVES],
+                        identity[:],
                     )
             image_t[s] = img_t
-            if k == CHUNK - 1 and c + RING < CHUNKS:
-                load_image(c + RING)
+            if k == CHUNK - 1 and c + IMAGE_RING < CHUNKS:
+                load_image(c + IMAGE_RING)
 
         def products(s):
             x = x_tiles[s]
-            y = y_tiles[s]
-            nc.vector.tensor_tensor(out=x[:], in0=image_t[s][:], in1=x[:], op=ALU.mult)
             nc.vector.scalar_tensor_tensor(
-                out=y[:], in0=image_t[s][:], scalar=1.0, in1=y[:], op0=ALU.subtract, op1=ALU.mult
+                out=x[:], in0=image_t[s][:], scalar=-1.0, in1=x[:], op0=ALU.mult, op1=ALU.mult
             )
-            nc.gpsimd.tensor_tensor(out=y[:], in0=y[:], in1=x[:], op=ALU.subtract)
 
         def transpose_loss(s):
-            loss_t[s] = []
-            for half in range(HALVES):
-                back = psum_back.tile([P, TOKEN_TILES, P], F32, tag="back")
-                for m in range(TOKEN_TILES):
-                    nc.tensor.transpose(back[:, m, :], y_tiles[s][:, half, m * P : (m + 1) * P], identity_f32[:])
-                loss_t[s].append(back)
+            back = psum_back.tile([P, TOKEN_TILES, P], F32, tag="back")
+            x = x_tiles[s]
+            for m in range(TOKEN_TILES):
+                tokens = slice(m * P, (m + 1) * P)
+                terms = (y_tiles[s][:, tokens], x[:, 0, tokens], x[:, 1, tokens])
+                for i, term in enumerate(terms):
+                    nc.tensor.matmul(
+                        out=back[:, m, :], lhsT=term, rhs=identity_f32[:],
+                        is_transpose=True, start=i == 0, stop=i == len(terms) - 1,
+                    )
+            loss_t[s] = back
 
         def row_sums(s):
-            for half in range(HALVES):
-                g = (HALVES * s + half) * (P // ROW)
-                nc.vector.tensor_reduce(
-                    out=loss[:, :, g : g + P // ROW],
-                    in_=loss_t[s][half][:].rearrange("p m (g w) -> p m g w", w=ROW),
-                    axis=AXIS.X,
-                    op=ALU.add,
-                )
-            if (s + 1) % BATCH == 0:
-                done = slice((s + 1 - BATCH) * SLAB // ROW, (s + 1) * SLAB // ROW)
+            g = SLAB // ROW
+            nc.vector.tensor_reduce(
+                out=loss[:, :, g * s : g * (s + 1)],
+                in_=loss_t[s][:].rearrange("p m (g w) -> p m g w", g=g),
+                axis=AXIS.X,
+                op=ALU.add,
+            )
+            if (s + 1) % 8 == 0:
+                done = slice(g * (s - 7), g * (s + 1))
                 nc.sync.dma_start(out=out_v[:, :, done], in_=loss[:, :, done])
 
-        for s in range(BATCH):
-            sigmoids(s)
-            one_minus(s)
-        transpose_image(0)
-        def slabs_ahead(batch, k):
-            if batch + 1 < BATCHES and 0 <= k - SIGMOID_FROM < SIGMOID_STEPS:
-                first = (batch + 1) * BATCH + (k - SIGMOID_FROM) * SIGMOID_SLABS
-                return list(range(first, first + SIGMOID_SLABS))
-            return []
+        def step(s):
+            if s + 1 < SLABS:
+                transpose_image(s + 1)
+            products(s)
+            if s >= 2:
+                row_sums(s - 2)
+            if s >= 1:
+                transpose_loss(s - 1)
 
-        for batch in range(BATCHES):
-            for k in range(BATCH):
-                logs(batch * BATCH + k)
-            for k in range(BATCH):
-                s = batch * BATCH + k
-                ahead = slabs_ahead(batch, k)
-                for a in ahead[:1]:
+        for s in range(Z_LEAD):
+            products_z(s)
+        first = 0
+        for s in range(BATCHES[0]):
+            sigmoids(s)
+            if s >= 1:
+                pair(s - 1)
+        pair(BATCHES[0] - 1)
+        transpose_image(0)
+        for n, size in enumerate(BATCHES):
+            ahead = BATCHES[n + 1] if n + 1 < len(BATCHES) else 0
+            slots = size + ahead
+            done = 0
+            for q in range(slots):
+                if q < size:
+                    logs(first + q)
+                else:
+                    a = first + q
                     sigmoids(a)
-                if s + 1 < SLABS:
-                    transpose_image(s + 1)
-                for a in ahead[1:]:
-                    sigmoids(a)
-                products(s)
-                for a in slabs_ahead(batch, k - 1):
-                    one_minus(a)
-                if s >= 2:
-                    row_sums(s - 2)
-                if s >= 1:
-                    transpose_loss(s - 1)
+                    if q > size:
+                        pair(a - 1)
+                while done < (q + 1) * size // slots:
+                    step(first + done)
+                    done += 1
+            if ahead:
+                pair(first + slots - 1)
+            first += size
         row_sums(SLABS - 2)
         transpose_loss(SLABS - 1)
         row_sums(SLABS - 1)

@@ -22,24 +22,27 @@ HIDDEN = 512
 FEATURES = 12288
 ROW = 64
 OUTPUTS = FEATURES // ROW
-HALVES = 2
-SLAB = HALVES * P
+PARTS = 4
+SLAB = PARTS * P
 SLABS = FEATURES // SLAB
-BATCHES = (6, 12, 14, 11, 5)
-LIVE = 17
-CHUNK = 4
+GROUPS = SLAB // ROW
+BATCHES = (3, 6, 7, 6, 2)
+LIVE = 9
+CHUNK = 2
 CHUNKS = SLABS // CHUNK
 RAW_RING = 3
 WORDS_RING = 3
 IMAGE_RING = 4
+STORE = 4
 Z_BANKS = 4
-Z_LEAD = Z_BANKS // HALVES
 
 EPS = 1e-9
 D = EPS / (1.0 + EPS)
 ODDS = 1.0 / D - D
 A_SCALE = ODDS / (1.0 + 2.0 * EPS)
 A_SHIFT = (1.0 + D) / ODDS
+QUADS = ROW // PARTS
+LOST = QUADS * 2.0 * math.log(A_SCALE)
 SELU_ALPHA = 1.6732632423543772848170429916717
 SELU_SCALE = 1.0507009873554804934193349852946
 
@@ -63,6 +66,7 @@ def tile_decoder_kernel(
         keep = stack.enter_context(tc.tile_pool(name="keep", bufs=1))
         x_pool = stack.enter_context(tc.tile_pool(name="x_pool", bufs=LIVE))
         y_pool = stack.enter_context(tc.tile_pool(name="y_pool", bufs=LIVE))
+        pair_pool = stack.enter_context(tc.tile_pool(name="pair_pool", bufs=3))
         raw_pool = stack.enter_context(tc.tile_pool(name="raw_pool", bufs=RAW_RING))
         words_pool = stack.enter_context(tc.tile_pool(name="words_pool", bufs=WORDS_RING))
         image_pool = stack.enter_context(tc.tile_pool(name="image_pool", bufs=IMAGE_RING))
@@ -76,11 +80,11 @@ def tile_decoder_kernel(
         bh_rows = keep.tile([P, HIDDEN], BF16)
         b1_all = keep.tile([P, HIDDEN], BF16)
         b2_rows = keep.tile([P, SLAB], BF16)
-        b2_t = keep.tile([P, HALVES, P], F32)
+        b2_t = keep.tile([P, PARTS, P], F32)
         w1_words = keep.tile([P, HIDDEN * PACK], U8, align_bytes=64)
         w1_plane = keep.tile([P, HIDDEN], U8, align_bytes=64)
         w2_raw_plane = keep.tile([P, FEATURES], U8, align_bytes=64)
-        w2_plane = keep.tile([P, SLABS, HALVES, P], U8, align_bytes=64)
+        w2_plane = keep.tile([P, SLABS, PARTS, P], U8, align_bytes=64)
         h_grouped = keep.tile([P, TOKEN_TILES, P, PACK], BF16, align_bytes=64)
         h_words = keep.tile([P, TOKEN_TILES, P], U32, align_bytes=64)
         h_plane = keep.tile([P, TOKEN_TILES, P], U8, align_bytes=64)
@@ -132,14 +136,14 @@ def tile_decoder_kernel(
             image_chunks[c] = img
 
         def split_words(c):
-            words = words_pool.tile([P, CHUNK, HALVES, P], U32, align_bytes=64)
+            words = words_pool.tile([P, CHUNK, PARTS, P], U32, align_bytes=64)
             nc.vector.tensor_copy(
-                out=words[:].bitcast(I32), in_=raw_chunks[c][:].rearrange("p (s i j) -> p s j i", j=HALVES, i=P)
+                out=words[:].bitcast(I32), in_=raw_chunks[c][:].rearrange("p (s i j) -> p s j i", j=PARTS, i=P)
             )
             slabs = slice(c * CHUNK, (c + 1) * CHUNK)
             nc.gpsimd.tensor_copy(
                 out=w2_plane[:, slabs, :, :],
-                in_=w2_raw_plane[:].rearrange("p (s i j) -> p s j i", j=HALVES, i=P)[:, slabs, :, :],
+                in_=w2_raw_plane[:].rearrange("p (s i j) -> p s j i", j=PARTS, i=P)[:, slabs, :, :],
             )
             w2_chunks[c] = words
             if c + RAW_RING < CHUNKS:
@@ -154,9 +158,9 @@ def tile_decoder_kernel(
         for m in range(TOKEN_TILES):
             nc.tensor.transpose(cat_ps[:, m * P : (m + 1) * P], cat[:, m, :], identity[:])
         nc.vector.tensor_copy(out=cat_t[:], in_=cat_ps[:])
-        b2_ps = psum_t.tile([P, HALVES, P], BF16, tag="transposed")
-        for j in range(HALVES):
-            nc.tensor.transpose(b2_ps[:, j, :], b2_rows[:, j::HALVES], identity[:])
+        b2_ps = psum_t.tile([P, PARTS, P], BF16, tag="transposed")
+        for j in range(PARTS):
+            nc.tensor.transpose(b2_ps[:, j, :], b2_rows[:, j::PARTS], identity[:])
         nc.vector.tensor_scalar_add(b2_t[:], b2_ps[:], math.log(D))
 
         wh_v = wh[:].rearrange("k (p j) -> k j p", j=PACK)
@@ -253,44 +257,47 @@ def tile_decoder_kernel(
         y_tiles = {}
         image_t = {}
         loss_t = {}
+        pair_tiles = {}
 
-        def products_z(s):
+        def product_z(s, j):
             c, k = divmod(s, CHUNK)
-            if k == 0 and c + 1 < CHUNKS:
+            if k == 0 and j == 0 and c + 1 < CHUNKS:
                 split_words(c + 1)
-            for half in range(HALVES):
-                z = psum_z.tile([P, TOKENS], F32, tag="z")
-                nc.tensor.matmul_mx(
-                    out=z[:],
-                    lhsT=w2_chunks[c][:, k, half, :].bitcast(FP8X4),
-                    lhsT_scale=w2_plane[:, s, half, :],
-                    rhs=t_words[:].bitcast(FP8X4),
-                    rhs_scale=t_plane[:],
-                    start=True,
-                    stop=True,
-                )
-                z_tiles[s, half] = z
+            z = psum_z.tile([P, TOKENS], F32, tag="z")
+            nc.tensor.matmul_mx(
+                out=z[:],
+                lhsT=w2_chunks[c][:, k, j, :].bitcast(FP8X4),
+                lhsT_scale=w2_plane[:, s, j, :],
+                rhs=t_words[:].bitcast(FP8X4),
+                rhs_scale=t_plane[:],
+                start=True,
+                stop=True,
+            )
+            z_tiles[s, j] = z
 
         def sigmoids(s):
-            x = x_pool.tile([P, HALVES, TOKENS], F32, tag="x")
-            for half in range(HALVES):
+            x = x_pool.tile([P, PARTS, TOKENS], F32, tag="x")
+            for j in range(PARTS):
                 nc.scalar.activation(
-                    out=x[:, half, :], in_=z_tiles[s, half][:], func=FUNC.Sigmoid, bias=b2_t[:, half, s : s + 1]
+                    out=x[:, j, :], in_=z_tiles[s, j][:], func=FUNC.Sigmoid, bias=b2_t[:, j, s : s + 1]
                 )
+                if s + 1 < SLABS:
+                    product_z(s + 1, j)
             x_tiles[s] = x
-            if s + Z_LEAD < SLABS:
-                products_z(s + Z_LEAD)
-            y = y_pool.tile([P, TOKENS], F32, tag="y")
+            pairs = pair_pool.tile([P, PARTS // 2, TOKENS], F32, tag="pairs")
             nc.gpsimd.tensor_scalar(
-                out=y[:], in0=x[:, 1, :], scalar1=1.0, scalar2=A_SHIFT, op0=ALU.mult, op1=ALU.add
+                out=pairs[:], in0=x[:, 1::2, :], scalar1=1.0, scalar2=A_SHIFT, op0=ALU.mult, op1=ALU.add
             )
-            y_tiles[s] = y
+            pair_tiles[s] = pairs
 
-        def pair(s):
-            y = y_tiles[s]
+        def quads(s):
+            pairs = pair_tiles[s]
             nc.vector.scalar_tensor_tensor(
-                out=y[:], in0=x_tiles[s][:, 0, :], scalar=A_SHIFT, in1=y[:], op0=ALU.add, op1=ALU.mult
+                out=pairs[:], in0=x_tiles[s][:, 0::2, :], scalar=A_SHIFT, in1=pairs[:], op0=ALU.add, op1=ALU.mult
             )
+            y = y_pool.tile([P, TOKENS], F32, tag="y")
+            nc.gpsimd.tensor_tensor(out=y[:], in0=pairs[:, 0, :], in1=pairs[:, 1, :], op=ALU.mult)
+            y_tiles[s] = y
 
         def logs(s):
             x = x_tiles[s]
@@ -298,69 +305,69 @@ def tile_decoder_kernel(
             nc.scalar.activation(out=x[:], in_=x[:], func=FUNC.Ln, scale=ODDS, bias=D)
             nc.scalar.activation(out=y[:], in_=y[:], func=FUNC.Ln, scale=A_SCALE * A_SCALE)
 
-        def transpose_image(s):
+        def transpose_image(s, h):
             c, k = divmod(s, CHUNK)
-            img_t = psum_t.tile([P, HALVES, TOKENS], BF16, tag="transposed")
-            for half in range(HALVES):
+            img_t = psum_t.tile([P, 2, TOKENS], BF16, tag="transposed")
+            for i in range(2):
                 for m in range(TOKEN_TILES):
                     nc.tensor.transpose(
-                        img_t[:, half, m * P : (m + 1) * P],
-                        image_chunks[c][:, m, k * SLAB + half : (k + 1) * SLAB : HALVES],
+                        img_t[:, i, m * P : (m + 1) * P],
+                        image_chunks[c][:, m, k * SLAB + 2 * h + i : (k + 1) * SLAB : PARTS],
                         identity[:],
                     )
-            image_t[s] = img_t
-            if k == CHUNK - 1 and c + IMAGE_RING < CHUNKS:
+            image_t[s, h] = img_t
+            if h == 1 and k == CHUNK - 1 and c + IMAGE_RING < CHUNKS:
                 load_image(c + IMAGE_RING)
 
-        def products(s):
-            x = x_tiles[s]
+        def products(s, h):
+            x = x_tiles[s][:, 2 * h : 2 * h + 2, :]
             nc.vector.scalar_tensor_tensor(
-                out=x[:], in0=image_t[s][:], scalar=-1.0, in1=x[:], op0=ALU.mult, op1=ALU.mult
+                out=x, in0=image_t[s, h][:], scalar=-1.0, in1=x, op0=ALU.mult, op1=ALU.mult
             )
 
-        def transpose_loss(s):
-            back = psum_back.tile([P, TOKEN_TILES, P], F32, tag="back")
-            x = x_tiles[s]
-            for m in range(TOKEN_TILES):
+        def transpose_loss(s, h):
+            if h == 0:
+                loss_t[s] = psum_back.tile([P, TOKEN_TILES, P], F32, tag="back", name="back")
+            for m in (2 * h, 2 * h + 1):
                 tokens = slice(m * P, (m + 1) * P)
-                terms = (y_tiles[s][:, tokens], x[:, 0, tokens], x[:, 1, tokens])
+                terms = [y_tiles[s][:, tokens]] + [x_tiles[s][:, j, tokens] for j in range(PARTS)]
                 for i, term in enumerate(terms):
                     nc.tensor.matmul(
-                        out=back[:, m, :], lhsT=term, rhs=identity_f32[:],
+                        out=loss_t[s][:, m, :], lhsT=term, rhs=identity_f32[:],
                         is_transpose=True, start=i == 0, stop=i == len(terms) - 1,
                     )
-            loss_t[s] = back
 
         def row_sums(s):
-            g = SLAB // ROW
             nc.vector.tensor_reduce(
-                out=loss[:, :, g * s : g * (s + 1)],
-                in_=loss_t[s][:].rearrange("p m (g w) -> p m g w", g=g),
+                out=loss[:, :, GROUPS * s : GROUPS * (s + 1)],
+                in_=loss_t[s][:].rearrange("p m (g w) -> p m g w", g=GROUPS),
                 axis=AXIS.X,
                 op=ALU.add,
             )
-            if (s + 1) % 8 == 0:
-                done = slice(g * (s - 7), g * (s + 1))
+            if (s + 1) % STORE == 0:
+                done = slice(GROUPS * (s + 1 - STORE), GROUPS * (s + 1))
+                nc.vector.tensor_scalar_add(loss[:, :, done], loss[:, :, done], LOST)
                 nc.sync.dma_start(out=out_v[:, :, done], in_=loss[:, :, done])
 
-        def step(s):
-            if s + 1 < SLABS:
-                transpose_image(s + 1)
-            products(s)
-            if s >= 2:
-                row_sums(s - 2)
+        def step(t):
+            s, h = divmod(t, 2)
+            if t + 1 < 2 * SLABS:
+                transpose_image(*divmod(t + 1, 2))
+            products(s, h)
             if s >= 1:
-                transpose_loss(s - 1)
+                transpose_loss(s - 1, h)
+            if s >= 2 and h == 0:
+                row_sums(s - 2)
 
-        for s in range(Z_LEAD):
-            products_z(s)
-        first = 0
+        for j in range(PARTS):
+            product_z(0, j)
         for s in range(BATCHES[0]):
             sigmoids(s)
             if s >= 1:
-                pair(s - 1)
-        pair(BATCHES[0] - 1)
-        transpose_image(0)
+                quads(s - 1)
+        quads(BATCHES[0] - 1)
+        transpose_image(0, 0)
+        first = 0
         for n, size in enumerate(BATCHES):
             ahead = BATCHES[n + 1] if n + 1 < len(BATCHES) else 0
             slots = size + ahead
@@ -369,16 +376,16 @@ def tile_decoder_kernel(
                 if q < size:
                     logs(first + q)
                 else:
-                    a = first + q
-                    sigmoids(a)
+                    sigmoids(first + q)
                     if q > size:
-                        pair(a - 1)
-                while done < (q + 1) * size // slots:
-                    step(first + done)
+                        quads(first + q - 1)
+                while done < (q + 1) * 2 * size // slots:
+                    step(2 * first + done)
                     done += 1
             if ahead:
-                pair(first + slots - 1)
+                quads(first + slots - 1)
             first += size
         row_sums(SLABS - 2)
-        transpose_loss(SLABS - 1)
+        for h in range(2):
+            transpose_loss(SLABS - 1, h)
         row_sums(SLABS - 1)

@@ -15,6 +15,7 @@ FUNC = mybir.ActivationFunctionType
 AXIS = mybir.AxisListType
 
 P = 128
+SCALE_ROWS = 16
 PACK = 4
 TOKENS = 512
 TOKEN_TILES = TOKENS // P
@@ -33,6 +34,8 @@ CHUNKS = SLABS // CHUNK
 RAW_RING = 3
 WORDS_RING = 3
 IMAGE_RING = 4
+STRETCHES = P // SCALE_ROWS
+STRETCH = SLABS // STRETCHES
 STORE = 4
 Z_BANKS = 4
 
@@ -78,12 +81,16 @@ def tile_decoder_kernel(
         cat_t = keep.tile([P, TOKENS], BF16)
         wh = keep.tile([P, HIDDEN], BF16)
         bh_rows = keep.tile([P, HIDDEN], BF16)
-        b1_all = keep.tile([P, HIDDEN], BF16)
+        b1_t = keep.tile([P, PACK], BF16)
+        b1_scaled = keep.tile([P, PACK], F32)
         b2_rows = keep.tile([P, SLAB], BF16)
         b2_t = keep.tile([P, PARTS, P], F32)
-        w1_words = keep.tile([P, HIDDEN * PACK], U8, align_bytes=64)
-        w1_plane = keep.tile([P, HIDDEN], U8, align_bytes=64)
-        w2_raw_plane = keep.tile([P, FEATURES], U8, align_bytes=64)
+        w1_raw = keep.tile([P, HIDDEN], I32)
+        w1_raw_plane = keep.tile([P, HIDDEN], U8, align_bytes=64)
+        w1_words = keep.tile([P, PACK, P], U32, align_bytes=64)
+        w1_plane = keep.tile([P, PACK, P], U8, align_bytes=64)
+        w2_scales = keep.tile([P, STRETCH * SLAB], U8, align_bytes=64)
+        w2_split_scales = keep.tile([P, STRETCH, PARTS, P], U8, align_bytes=64)
         w2_plane = keep.tile([P, SLABS, PARTS, P], U8, align_bytes=64)
         h_grouped = keep.tile([P, TOKEN_TILES, P, PACK], BF16, align_bytes=64)
         h_words = keep.tile([P, TOKEN_TILES, P], U32, align_bytes=64)
@@ -94,12 +101,13 @@ def tile_decoder_kernel(
         identity = keep.tile([P, P], BF16)
         identity_f32 = keep.tile([P, P], F32)
         ones = keep.tile([P, P], BF16)
+        warm = keep.tile([P, 1], F32)
         loss = keep.tile([P, TOKEN_TILES, OUTPUTS], F32)
 
         nc.vector.memset(bh_rows[:], 0.0)
         nc.vector.memset(b2_rows[:], 0.0)
-        nc.vector.memset(w1_plane[:].bitcast(I32), 0)
-        nc.vector.memset(w2_raw_plane[:].bitcast(I32), 0)
+        nc.vector.memset(w1_raw_plane[:].bitcast(I32), 0)
+        nc.vector.memset(w2_plane[:].rearrange("p s j i -> p (s j i)").bitcast(I32), 0)
         make_identity(nc, identity[:])
         make_identity(nc, identity_f32[:])
         nc.gpsimd.memset(ones[:], 1.0)
@@ -107,18 +115,19 @@ def tile_decoder_kernel(
         nc.sync.dma_start(out=cat[:, :, 0:32], in_=digits_v)
         nc.sync.dma_start(out=cat[:, :, 32:P], in_=styles_v)
         nc.sync.dma_start(out=wh[:], in_=W_h)
-        nc.sync.dma_start(out=w1_words[:].bitcast(I32), in_=w1_bytes.bitcast(I32))
         nc.sync.dma_start(out=bh_rows[0:1, :], in_=b_h.rearrange("(o n) -> o n", o=1))
-        nc.sync.dma_start(out=b1_all[:], in_=b1.partition_broadcast(P))
+        nc.sync.dma_start(out=w1_raw[:], in_=w1_bytes.bitcast(I32))
+        nc.sync.dma_start(out=b1_t[:], in_=b1.rearrange("(p j) -> p j", j=PACK))
         nc.sync.dma_start(out=b2_rows[0:SLABS, :], in_=b2.rearrange("(s f) -> s f", f=SLAB))
         for quadrant in range(4):
             rows = slice(4 * quadrant, 4 * quadrant + 4)
             live = slice(32 * quadrant, 32 * quadrant + 4)
-            nc.sync.dma_start(out=w1_plane[live, :].bitcast(I32), in_=W1_scales[0, rows, :].bitcast(I32))
-        for quadrant in range(4):
-            rows = slice(4 * quadrant, 4 * quadrant + 4)
-            live = slice(32 * quadrant, 32 * quadrant + 4)
-            nc.sync.dma_start(out=w2_raw_plane[live, :].bitcast(I32), in_=W2_scales[0, rows, :].bitcast(I32))
+            nc.sync.dma_start(out=w1_raw_plane[live, :].bitcast(I32), in_=W1_scales[0, rows, :].bitcast(I32))
+        for b in range(STRETCHES):
+            nc.sync.dma_start(
+                out=w2_scales[b * SCALE_ROWS : (b + 1) * SCALE_ROWS, :].bitcast(I32),
+                in_=W2_scales[0, :, b * STRETCH * SLAB : (b + 1) * STRETCH * SLAB].bitcast(I32),
+            )
 
         raw_chunks = {}
         w2_chunks = {}
@@ -138,31 +147,41 @@ def tile_decoder_kernel(
         def split_words(c):
             words = words_pool.tile([P, CHUNK, PARTS, P], U32, align_bytes=64)
             nc.vector.tensor_copy(
-                out=words[:].bitcast(I32), in_=raw_chunks[c][:].rearrange("p (s i j) -> p s j i", j=PARTS, i=P)
-            )
-            slabs = slice(c * CHUNK, (c + 1) * CHUNK)
-            nc.gpsimd.tensor_copy(
-                out=w2_plane[:, slabs, :, :],
-                in_=w2_raw_plane[:].rearrange("p (s i j) -> p s j i", j=PARTS, i=P)[:, slabs, :, :],
+                out=words[:].bitcast(I32).rearrange("p s j i -> p s i j"),
+                in_=raw_chunks[c][:].rearrange("p (s i j) -> p s i j", j=PARTS, i=P),
             )
             w2_chunks[c] = words
             if c + RAW_RING < CHUNKS:
                 load_words(c + RAW_RING)
 
-        for c in range(RAW_RING):
+        def split_scales():
+            nc.gpsimd.tensor_copy(
+                out=w2_split_scales[:].rearrange("p s j i -> p s i j"),
+                in_=w2_scales[:].rearrange("p (s i j) -> p s i j", j=PARTS, i=P),
+            )
+            split = w2_split_scales[:].rearrange("p s j i -> p (s j i)")
+            plane = w2_plane[:].rearrange("p s j i -> p (s j i)")
+            for b in range(STRETCHES):
+                for quadrant in range(4):
+                    first = b * SCALE_ROWS + 4 * quadrant
+                    nc.sync.dma_start(
+                        out=plane[32 * quadrant : 32 * quadrant + 4, b * STRETCH * SLAB : (b + 1) * STRETCH * SLAB].bitcast(I32),
+                        in_=split[first : first + 4, :].bitcast(I32),
+                    )
+
+        nc.gpsimd.tensor_copy(out=w1_plane[:], in_=w1_raw_plane[:].rearrange("k (p j) -> k j p", j=PACK))
+        load_words(0)
+        load_image(0)
+        split_scales()
+        for c in range(1, RAW_RING):
             load_words(c)
-        for c in range(IMAGE_RING):
+        for c in range(1, IMAGE_RING):
             load_image(c)
 
         cat_ps = psum_t.tile([P, TOKENS], BF16, tag="transposed")
         for m in range(TOKEN_TILES):
             nc.tensor.transpose(cat_ps[:, m * P : (m + 1) * P], cat[:, m, :], identity[:])
         nc.vector.tensor_copy(out=cat_t[:], in_=cat_ps[:])
-        b2_ps = psum_t.tile([P, PARTS, P], BF16, tag="transposed")
-        for j in range(PARTS):
-            nc.tensor.transpose(b2_ps[:, j, :], b2_rows[:, j::PARTS], identity[:])
-        nc.vector.tensor_scalar_add(b2_t[:], b2_ps[:], math.log(D))
-
         wh_v = wh[:].rearrange("k (p j) -> k j p", j=PACK)
         bh_v = bh_rows[:].rearrange("k (p j) -> k j p", j=PACK)
 
@@ -170,9 +189,16 @@ def tile_decoder_kernel(
         t_ps = {}
         u = {}
         e = {}
-        r = {}
-        t_sb = {}
-        t_ps_t = {}
+
+        def prepare_w1():
+            nc.vector.tensor_copy(out=w1_words[:].bitcast(I32), in_=w1_raw[:].rearrange("k (p j) -> k j p", j=PACK))
+            nc.vector.tensor_scalar_mul(b1_scaled[:], b1_t[:], SELU_SCALE)
+
+        def prepare_b2():
+            b2_ps = psum_t.tile([P, PARTS, P], BF16, tag="transposed")
+            for j in range(PARTS):
+                nc.tensor.transpose(b2_ps[:, j, :], b2_rows[:, j::PARTS], identity[:])
+            nc.vector.tensor_scalar_add(b2_t[:], b2_ps[:], math.log(D))
 
         def hidden_matmuls(m):
             h_ps[m] = psum_z.tile([P, PACK, P], F32, tag="z", name="h_ps")
@@ -196,44 +222,42 @@ def tile_decoder_kernel(
                 scales=h_plane[:, m, :],
                 in_=h_grouped[:, m, :, :].rearrange("p t j -> p (t j)"),
             )
-            t_ps[m] = psum_z.tile([P, HIDDEN], F32, tag="z", name="t_ps")
-            nc.tensor.matmul_mx(
-                out=t_ps[m][:],
-                lhsT=h_words[:, m, :].bitcast(FP8X4),
-                lhsT_scale=h_plane[:, m, :],
-                rhs=w1_words[:].bitcast(FP8X4),
-                rhs_scale=w1_plane[:],
-                start=True,
-                stop=True,
-            )
+            t_ps[m] = psum_z.tile([P, PACK, P], F32, tag="z", name="t_ps")
+            for j in range(PACK):
+                nc.tensor.matmul_mx(
+                    out=t_ps[m][:, j, :],
+                    lhsT=w1_words[:, j, :].bitcast(FP8X4),
+                    lhsT_scale=w1_plane[:, j, :],
+                    rhs=h_words[:, m, :].bitcast(FP8X4),
+                    rhs_scale=h_plane[:, m, :],
+                    start=True,
+                    stop=True,
+                )
 
         def add_b1(m):
-            u[m] = x_pool.tile([P, HIDDEN], F32, tag="x", name="u")
-            nc.vector.tensor_tensor(out=u[m][:], in0=t_ps[m][:], in1=b1_all[:], op=ALU.add)
-
-        def selu_on_scalar(m):
-            e[m] = y_pool.tile([P, HIDDEN], F32, tag="y", name="e")
-            nc.scalar.activation(out=e[m][:], in_=u[m][:], func=FUNC.Exp)
-            r[m] = x_pool.tile([P, HIDDEN], F32, tag="x", name="r")
-            nc.scalar.activation(out=r[m][:], in_=u[m][:], func=FUNC.Relu, scale=SELU_SCALE)
-
-        def selu_on_vector(m):
-            nc.vector.tensor_scalar(
-                out=e[m][:], in0=e[m][:], scalar1=1.0, scalar2=SELU_SCALE * SELU_ALPHA,
-                op0=ALU.min, op1=ALU.mult,
-            )
-            t_sb[m] = keep.tile([P, HIDDEN], BF16, tag="t_sb", bufs=2, name="t_sb")
+            u[m] = x_pool.tile([P, PACK, P], F32, tag="x", name="u")
             nc.vector.scalar_tensor_tensor(
-                out=t_sb[m][:], in0=e[m][:], scalar=-SELU_SCALE * SELU_ALPHA, in1=r[m][:],
-                op0=ALU.add, op1=ALU.add,
+                out=u[m][:], in0=t_ps[m][:], scalar=SELU_SCALE,
+                in1=b1_scaled[:].unsqueeze(2).to_broadcast([P, PACK, P]), op0=ALU.mult, op1=ALU.add,
             )
-            t_v = t_sb[m][:].rearrange("t (p j) -> t j p", j=PACK)
-            t_ps_t[m] = psum_t.tile([P, PACK, P], BF16, tag="transposed", name="t_ps_t")
-            for j in range(PACK):
-                nc.tensor.transpose(t_ps_t[m][:, j, :], t_v[:, j, :], identity[:])
 
-        def group_t(m):
-            nc.scalar.copy(out=t_grouped[:, m, :, :], in_=t_ps_t[m][:].rearrange("p j t -> p t j"))
+        def exponential(m):
+            e[m] = y_pool.tile([P, PACK, P], F32, tag="y", name="e")
+            nc.scalar.activation(
+                out=e[m][:], in_=u[m][:], func=FUNC.Exp, scale=1.0 / SELU_SCALE, bias=math.log(SELU_SCALE * SELU_ALPHA)
+            )
+
+        def clamp(m):
+            nc.vector.tensor_scalar(
+                out=e[m][:], in0=e[m][:], scalar1=SELU_SCALE * SELU_ALPHA, scalar2=-SELU_SCALE * SELU_ALPHA,
+                op0=ALU.min, op1=ALU.add,
+            )
+
+        def selu(m):
+            nc.vector.scalar_tensor_tensor(
+                out=t_grouped[:, m, :, :], in0=u[m][:].rearrange("p j t -> p t j"), scalar=0.0,
+                in1=e[m][:].rearrange("p j t -> p t j"), op0=ALU.max, op1=ALU.add,
+            )
 
         def quantise_t(m):
             nc.vector.quantize_mx(
@@ -243,14 +267,16 @@ def tile_decoder_kernel(
             )
 
         stages = [
-            hidden_matmuls, relu, bottleneck_matmul, add_b1,
-            selu_on_scalar, selu_on_vector, group_t, quantise_t,
+            hidden_matmuls, relu, bottleneck_matmul, add_b1, exponential, clamp, selu, quantise_t,
         ]
-        split_words(0)
+        between = {1: prepare_w1, 5: prepare_b2, 6: lambda: split_words(0)}
         for tick in range(TOKEN_TILES + len(stages) - 1):
             for depth in reversed(range(len(stages))):
                 if 0 <= tick - depth < TOKEN_TILES:
                     stages[depth](tick - depth)
+            if tick in between:
+                between[tick]()
+        nc.scalar.activation(out=warm[:], in_=ones[:, 0:1], func=FUNC.Sigmoid)
 
         z_tiles = {}
         x_tiles = {}
@@ -307,14 +333,15 @@ def tile_decoder_kernel(
 
         def transpose_image(s, h):
             c, k = divmod(s, CHUNK)
-            img_t = psum_t.tile([P, 2, TOKENS], BF16, tag="transposed")
-            for i in range(2):
-                for m in range(TOKEN_TILES):
-                    nc.tensor.transpose(
-                        img_t[:, i, m * P : (m + 1) * P],
-                        image_chunks[c][:, m, k * SLAB + 2 * h + i : (k + 1) * SLAB : PARTS],
-                        identity[:],
-                    )
+            words = image_chunks[c][:].rearrange("p m f -> p (m f)").bitcast(F32)
+            words = words.rearrange("p (m f) -> p m f", m=TOKEN_TILES)
+            img_t = psum_t.tile([P, TOKENS], F32, tag="transposed")
+            for m in range(TOKEN_TILES):
+                nc.tensor.transpose(
+                    img_t[:, m * P : (m + 1) * P],
+                    words[:, m, k * SLAB // 2 + h : (k + 1) * SLAB // 2 : 2],
+                    identity_f32[:],
+                )
             image_t[s, h] = img_t
             if h == 1 and k == CHUNK - 1 and c + IMAGE_RING < CHUNKS:
                 load_image(c + IMAGE_RING)
@@ -322,7 +349,7 @@ def tile_decoder_kernel(
         def products(s, h):
             x = x_tiles[s][:, 2 * h : 2 * h + 2, :]
             nc.vector.scalar_tensor_tensor(
-                out=x, in0=image_t[s, h][:], scalar=-1.0, in1=x, op0=ALU.mult, op1=ALU.mult
+                out=x, in0=image_t[s, h][:].bitcast(BF16).rearrange("p (t e) -> p e t", e=2), scalar=-1.0, in1=x, op0=ALU.mult, op1=ALU.mult
             )
 
         def transpose_loss(s, h):

@@ -27,13 +27,13 @@ PARTS = 4
 SLAB = PARTS * P
 SLABS = FEATURES // SLAB
 GROUPS = SLAB // ROW
-BATCHES = (3, 6, 7, 6, 2)
-LIVE = 9
+BATCHES = (4, 12, 8)
+LIVE = 14
 CHUNK = 2
 CHUNKS = SLABS // CHUNK
-RAW_RING = 3
+RAW_RING = 2
 WORDS_RING = 3
-IMAGE_RING = 4
+IMAGE_RING = 3
 STRETCHES = P // SCALE_ROWS
 STRETCH = SLABS // STRETCHES
 STORE = 4
@@ -92,10 +92,8 @@ def tile_decoder_kernel(
         w2_scales = keep.tile([P, STRETCH * SLAB], U8, align_bytes=64)
         w2_split_scales = keep.tile([P, STRETCH, PARTS, P], U8, align_bytes=64)
         w2_plane = keep.tile([P, SLABS, PARTS, P], U8, align_bytes=64)
-        h_grouped = keep.tile([P, TOKEN_TILES, P, PACK], BF16, align_bytes=64)
         h_words = keep.tile([P, TOKEN_TILES, P], U32, align_bytes=64)
         h_plane = keep.tile([P, TOKEN_TILES, P], U8, align_bytes=64)
-        t_grouped = keep.tile([P, TOKEN_TILES, P, PACK], BF16, align_bytes=64)
         t_words = keep.tile([P, TOKENS], U32, align_bytes=64)
         t_plane = keep.tile([P, TOKENS], U8, align_bytes=64)
         identity = keep.tile([P, P], BF16)
@@ -117,8 +115,6 @@ def tile_decoder_kernel(
         nc.sync.dma_start(out=wh[:], in_=W_h)
         nc.sync.dma_start(out=bh_rows[0:1, :], in_=b_h.rearrange("(o n) -> o n", o=1))
         nc.sync.dma_start(out=w1_raw[:], in_=w1_bytes.bitcast(I32))
-        nc.sync.dma_start(out=b1_t[:], in_=b1.rearrange("(p j) -> p j", j=PACK))
-        nc.sync.dma_start(out=b2_rows[0:SLABS, :], in_=b2.rearrange("(s f) -> s f", f=SLAB))
         for quadrant in range(4):
             rows = slice(4 * quadrant, 4 * quadrant + 4)
             live = slice(32 * quadrant, 32 * quadrant + 4)
@@ -154,29 +150,35 @@ def tile_decoder_kernel(
             if c + RAW_RING < CHUNKS:
                 load_words(c + RAW_RING)
 
-        def split_scales():
+        def split_scales(k):
             nc.gpsimd.tensor_copy(
-                out=w2_split_scales[:].rearrange("p s j i -> p s i j"),
-                in_=w2_scales[:].rearrange("p (s i j) -> p s i j", j=PARTS, i=P),
+                out=w2_split_scales[:, k, :, :].rearrange("p j i -> p i j"),
+                in_=w2_scales[:, k * SLAB : (k + 1) * SLAB].rearrange("p (i j) -> p i j", j=PARTS),
             )
+
+        def place_scales(b, k, count):
             split = w2_split_scales[:].rearrange("p s j i -> p (s j i)")
             plane = w2_plane[:].rearrange("p s j i -> p (s j i)")
-            for b in range(STRETCHES):
-                for quadrant in range(4):
-                    first = b * SCALE_ROWS + 4 * quadrant
-                    nc.sync.dma_start(
-                        out=plane[32 * quadrant : 32 * quadrant + 4, b * STRETCH * SLAB : (b + 1) * STRETCH * SLAB].bitcast(I32),
-                        in_=split[first : first + 4, :].bitcast(I32),
-                    )
+            source = slice(k * SLAB, (k + count) * SLAB)
+            target = slice((b * STRETCH + k) * SLAB, (b * STRETCH + k + count) * SLAB)
+            for quadrant in range(4):
+                first = b * SCALE_ROWS + 4 * quadrant
+                nc.sync.dma_start(
+                    out=plane[32 * quadrant : 32 * quadrant + 4, target].bitcast(I32),
+                    in_=split[first : first + 4, source].bitcast(I32),
+                )
 
         nc.gpsimd.tensor_copy(out=w1_plane[:], in_=w1_raw_plane[:].rearrange("k (p j) -> k j p", j=PACK))
+        for k in range(STRETCH):
+            split_scales(k)
         load_words(0)
+        nc.sync.dma_start(out=b1_t[:], in_=b1.rearrange("(p j) -> p j", j=PACK))
+        nc.sync.dma_start(out=b2_rows[0:SLABS, :], in_=b2.rearrange("(s f) -> s f", f=SLAB))
+        load_words(1)
+        place_scales(0, 0, 1)
+        place_scales(0, 1, STRETCH - 1)
         load_image(0)
-        split_scales()
-        for c in range(1, RAW_RING):
-            load_words(c)
-        for c in range(1, IMAGE_RING):
-            load_image(c)
+        place_scales(1, 0, STRETCH)
 
         cat_ps = psum_t.tile([P, TOKENS], BF16, tag="transposed")
         for m in range(TOKEN_TILES):
@@ -189,6 +191,10 @@ def tile_decoder_kernel(
         t_ps = {}
         u = {}
         e = {}
+        grouped = {}
+
+        def grouped_tile():
+            return keep.tile([P, P, PACK], BF16, tag="grouped", bufs=TOKEN_TILES, align_bytes=64, name="grouped")
 
         def prepare_w1():
             nc.vector.tensor_copy(out=w1_words[:].bitcast(I32), in_=w1_raw[:].rearrange("k (p j) -> k j p", j=PACK))
@@ -198,7 +204,7 @@ def tile_decoder_kernel(
             b2_ps = psum_t.tile([P, PARTS, P], BF16, tag="transposed")
             for j in range(PARTS):
                 nc.tensor.transpose(b2_ps[:, j, :], b2_rows[:, j::PARTS], identity[:])
-            nc.vector.tensor_scalar_add(b2_t[:], b2_ps[:], math.log(D))
+            nc.scalar.activation(out=b2_t[:], in_=b2_ps[:], func=FUNC.Identity, bias=math.log(D))
 
         def hidden_matmuls(m):
             h_ps[m] = psum_z.tile([P, PACK, P], F32, tag="z", name="h_ps")
@@ -212,15 +218,16 @@ def tile_decoder_kernel(
                 )
 
         def relu(m):
+            grouped[m] = grouped_tile()
             nc.scalar.activation(
-                out=h_grouped[:, m, :, :], in_=h_ps[m][:].rearrange("p j t -> p t j"), func=FUNC.Relu
+                out=grouped[m][:], in_=h_ps[m][:].rearrange("p j t -> p t j"), func=FUNC.Relu
             )
 
         def bottleneck_matmul(m):
             nc.vector.quantize_mx(
                 out=h_words[:, m, :].bitcast(FP8X4),
                 scales=h_plane[:, m, :],
-                in_=h_grouped[:, m, :, :].rearrange("p t j -> p (t j)"),
+                in_=grouped[m][:].rearrange("p t j -> p (t j)"),
             )
             t_ps[m] = psum_z.tile([P, PACK, P], F32, tag="z", name="t_ps")
             for j in range(PACK):
@@ -254,8 +261,9 @@ def tile_decoder_kernel(
             )
 
         def selu(m):
+            grouped[m] = grouped_tile()
             nc.vector.scalar_tensor_tensor(
-                out=t_grouped[:, m, :, :], in0=u[m][:].rearrange("p j t -> p t j"), scalar=0.0,
+                out=grouped[m][:], in0=u[m][:].rearrange("p j t -> p t j"), scalar=0.0,
                 in1=e[m][:].rearrange("p j t -> p t j"), op0=ALU.max, op1=ALU.add,
             )
 
@@ -263,7 +271,7 @@ def tile_decoder_kernel(
             nc.vector.quantize_mx(
                 out=t_words[:, m * P : (m + 1) * P].bitcast(FP8X4),
                 scales=t_plane[:, m * P : (m + 1) * P],
-                in_=t_grouped[:, m, :, :].rearrange("p t j -> p (t j)"),
+                in_=grouped[m][:].rearrange("p t j -> p (t j)"),
             )
 
         stages = [
@@ -276,6 +284,10 @@ def tile_decoder_kernel(
                     stages[depth](tick - depth)
             if tick in between:
                 between[tick]()
+        for c in range(1, IMAGE_RING):
+            load_image(c)
+        for b in range(2, STRETCHES):
+            place_scales(b, 0, STRETCH)
         nc.scalar.activation(out=warm[:], in_=ones[:, 0:1], func=FUNC.Sigmoid)
 
         z_tiles = {}
@@ -287,7 +299,7 @@ def tile_decoder_kernel(
 
         def product_z(s, j):
             c, k = divmod(s, CHUNK)
-            if k == 0 and j == 0 and c + 1 < CHUNKS:
+            if k == 1 and j == 0 and c + 1 < CHUNKS:
                 split_words(c + 1)
             z = psum_z.tile([P, TOKENS], F32, tag="z")
             nc.tensor.matmul_mx(

@@ -19,6 +19,7 @@ SCALE_ROWS = 16
 PACK = 4
 TOKENS = 512
 TOKEN_TILES = TOKENS // P
+TOKEN_HALVES = (slice(0, TOKENS // 2), slice(TOKENS // 2, TOKENS))
 HIDDEN = 512
 FEATURES = 12288
 ROW = 64
@@ -27,16 +28,18 @@ PARTS = 4
 SLAB = PARTS * P
 SLABS = FEATURES // SLAB
 GROUPS = SLAB // ROW
-BATCHES = (4, 12, 8)
+BATCHES = (10, 11, 3)
 LIVE = 14
 CHUNK = 2
 CHUNKS = SLABS // CHUNK
-RAW_RING = 2
+RAW_RING = 3
 WORDS_RING = 3
 IMAGE_RING = 3
 STRETCHES = P // SCALE_ROWS
 STRETCH = SLABS // STRETCHES
 STORE = 4
+SPLIT_LEAD = 3
+PLACE_LEAD = 5
 Z_BANKS = 4
 
 EPS = 1e-9
@@ -69,7 +72,7 @@ def tile_decoder_kernel(
         keep = stack.enter_context(tc.tile_pool(name="keep", bufs=1))
         x_pool = stack.enter_context(tc.tile_pool(name="x_pool", bufs=LIVE))
         y_pool = stack.enter_context(tc.tile_pool(name="y_pool", bufs=LIVE))
-        pair_pool = stack.enter_context(tc.tile_pool(name="pair_pool", bufs=3))
+        pair_pool = stack.enter_context(tc.tile_pool(name="pair_pool", bufs=2))
         raw_pool = stack.enter_context(tc.tile_pool(name="raw_pool", bufs=RAW_RING))
         words_pool = stack.enter_context(tc.tile_pool(name="words_pool", bufs=WORDS_RING))
         image_pool = stack.enter_context(tc.tile_pool(name="image_pool", bufs=IMAGE_RING))
@@ -115,6 +118,8 @@ def tile_decoder_kernel(
         nc.sync.dma_start(out=wh[:], in_=W_h)
         nc.sync.dma_start(out=bh_rows[0:1, :], in_=b_h.rearrange("(o n) -> o n", o=1))
         nc.sync.dma_start(out=w1_raw[:], in_=w1_bytes.bitcast(I32))
+        nc.sync.dma_start(out=b1_t[:], in_=b1.rearrange("(p j) -> p j", j=PACK))
+        nc.sync.dma_start(out=b2_rows[0:SLABS, :], in_=b2.rearrange("(s f) -> s f", f=SLAB))
         for quadrant in range(4):
             rows = slice(4 * quadrant, 4 * quadrant + 4)
             live = slice(32 * quadrant, 32 * quadrant + 4)
@@ -151,7 +156,7 @@ def tile_decoder_kernel(
                 load_words(c + RAW_RING)
 
         def split_scales(k):
-            nc.gpsimd.tensor_copy(
+            nc.vector.tensor_copy(
                 out=w2_split_scales[:, k, :, :].rearrange("p j i -> p i j"),
                 in_=w2_scales[:, k * SLAB : (k + 1) * SLAB].rearrange("p (i j) -> p i j", j=PARTS),
             )
@@ -168,17 +173,10 @@ def tile_decoder_kernel(
                     in_=split[first : first + 4, source].bitcast(I32),
                 )
 
-        nc.gpsimd.tensor_copy(out=w1_plane[:], in_=w1_raw_plane[:].rearrange("k (p j) -> k j p", j=PACK))
-        for k in range(STRETCH):
-            split_scales(k)
         load_words(0)
-        nc.sync.dma_start(out=b1_t[:], in_=b1.rearrange("(p j) -> p j", j=PACK))
-        nc.sync.dma_start(out=b2_rows[0:SLABS, :], in_=b2.rearrange("(s f) -> s f", f=SLAB))
         load_words(1)
-        place_scales(0, 0, 1)
-        place_scales(0, 1, STRETCH - 1)
+        load_words(2)
         load_image(0)
-        place_scales(1, 0, STRETCH)
 
         cat_ps = psum_t.tile([P, TOKENS], BF16, tag="transposed")
         for m in range(TOKEN_TILES):
@@ -197,7 +195,12 @@ def tile_decoder_kernel(
             return keep.tile([P, P, PACK], BF16, tag="grouped", bufs=TOKEN_TILES, align_bytes=64, name="grouped")
 
         def prepare_w1():
-            nc.vector.tensor_copy(out=w1_words[:].bitcast(I32), in_=w1_raw[:].rearrange("k (p j) -> k j p", j=PACK))
+            nc.vector.tensor_copy(
+                out=w1_words[:].bitcast(I32).rearrange("k j p -> k p j"), in_=w1_raw[:].rearrange("k (p j) -> k p j", j=PACK)
+            )
+            nc.vector.tensor_copy(
+                out=w1_plane[:].rearrange("k j p -> k p j"), in_=w1_raw_plane[:].rearrange("k (p j) -> k p j", j=PACK)
+            )
             nc.vector.tensor_scalar_mul(b1_scaled[:], b1_t[:], SELU_SCALE)
 
         def prepare_b2():
@@ -274,20 +277,28 @@ def tile_decoder_kernel(
                 in_=grouped[m][:].rearrange("p t j -> p (t j)"),
             )
 
-        stages = [
-            hidden_matmuls, relu, bottleneck_matmul, add_b1, exponential, clamp, selu, quantise_t,
-        ]
-        between = {1: prepare_w1, 5: prepare_b2, 6: lambda: split_words(0)}
+        stages = [relu, bottleneck_matmul, add_b1, exponential, clamp, selu, quantise_t]
+
+        def first_scales():
+            split_scales(0)
+            split_scales(1)
+            place_scales(0, 0, 2)
+
+        between = {3: prepare_b2, 4: first_scales, 5: lambda: split_words(0)}
+        for m in range(TOKEN_TILES):
+            hidden_matmuls(m)
+        prepare_w1()
         for tick in range(TOKEN_TILES + len(stages) - 1):
             for depth in reversed(range(len(stages))):
                 if 0 <= tick - depth < TOKEN_TILES:
                     stages[depth](tick - depth)
             if tick in between:
                 between[tick]()
+        split_scales(2)
+        place_scales(0, 2, 1)
+        place_scales(1, 0, STRETCH)
         for c in range(1, IMAGE_RING):
             load_image(c)
-        for b in range(2, STRETCHES):
-            place_scales(b, 0, STRETCH)
         nc.scalar.activation(out=warm[:], in_=ones[:, 0:1], func=FUNC.Sigmoid)
 
         z_tiles = {}
@@ -299,8 +310,6 @@ def tile_decoder_kernel(
 
         def product_z(s, j):
             c, k = divmod(s, CHUNK)
-            if k == 1 and j == 0 and c + 1 < CHUNKS:
-                split_words(c + 1)
             z = psum_z.tile([P, TOKENS], F32, tag="z")
             nc.tensor.matmul_mx(
                 out=z[:],
@@ -322,9 +331,11 @@ def tile_decoder_kernel(
                 if s + 1 < SLABS:
                     product_z(s + 1, j)
             x_tiles[s] = x
+
+        def factors(s):
             pairs = pair_pool.tile([P, PARTS // 2, TOKENS], F32, tag="pairs")
-            nc.gpsimd.tensor_scalar(
-                out=pairs[:], in0=x[:, 1::2, :], scalar1=1.0, scalar2=A_SHIFT, op0=ALU.mult, op1=ALU.add
+            nc.vector.tensor_scalar(
+                out=pairs[:], in0=x_tiles[s][:, 1::2, :], scalar1=1.0, scalar2=A_SHIFT, op0=ALU.mult, op1=ALU.add
             )
             pair_tiles[s] = pairs
 
@@ -333,15 +344,22 @@ def tile_decoder_kernel(
             nc.vector.scalar_tensor_tensor(
                 out=pairs[:], in0=x_tiles[s][:, 0::2, :], scalar=A_SHIFT, in1=pairs[:], op0=ALU.add, op1=ALU.mult
             )
+
+        def quad(s):
+            pairs = pair_tiles[s]
             y = y_pool.tile([P, TOKENS], F32, tag="y")
-            nc.gpsimd.tensor_tensor(out=y[:], in0=pairs[:, 0, :], in1=pairs[:, 1, :], op=ALU.mult)
+            nc.vector.tensor_tensor(out=y[:], in0=pairs[:, 0, :], in1=pairs[:, 1, :], op=ALU.mult)
             y_tiles[s] = y
 
         def logs(s):
             x = x_tiles[s]
             y = y_tiles[s]
-            nc.scalar.activation(out=x[:], in_=x[:], func=FUNC.Ln, scale=ODDS, bias=D)
+            if s < SLABS - 1:
+                nc.scalar.activation(out=x[:], in_=x[:], func=FUNC.Ln, scale=ODDS, bias=D)
             nc.scalar.activation(out=y[:], in_=y[:], func=FUNC.Ln, scale=A_SCALE * A_SCALE)
+            if s == SLABS - 1:
+                for half in TOKEN_HALVES:
+                    nc.scalar.activation(out=x[:, :, half], in_=x[:, :, half], func=FUNC.Ln, scale=ODDS, bias=D)
 
         def transpose_image(s, h):
             c, k = divmod(s, CHUNK)
@@ -358,11 +376,10 @@ def tile_decoder_kernel(
             if h == 1 and k == CHUNK - 1 and c + IMAGE_RING < CHUNKS:
                 load_image(c + IMAGE_RING)
 
-        def products(s, h):
-            x = x_tiles[s][:, 2 * h : 2 * h + 2, :]
-            nc.vector.scalar_tensor_tensor(
-                out=x, in0=image_t[s, h][:].bitcast(BF16).rearrange("p (t e) -> p e t", e=2), scalar=-1.0, in1=x, op0=ALU.mult, op1=ALU.mult
-            )
+        def products(s, h, tokens=slice(0, TOKENS)):
+            x = x_tiles[s][:, 2 * h : 2 * h + 2, tokens]
+            img = image_t[s, h][:].bitcast(BF16).rearrange("p (t e) -> p e t", e=2)[:, :, tokens]
+            nc.vector.scalar_tensor_tensor(out=x, in0=img, scalar=-1.0, in1=x, op0=ALU.mult, op1=ALU.mult)
 
         def transpose_loss(s, h):
             if h == 0:
@@ -376,17 +393,17 @@ def tile_decoder_kernel(
                         is_transpose=True, start=i == 0, stop=i == len(terms) - 1,
                     )
 
-        def row_sums(s):
+        def row_sums(s, tiles=slice(0, TOKEN_TILES)):
             nc.vector.tensor_reduce(
-                out=loss[:, :, GROUPS * s : GROUPS * (s + 1)],
-                in_=loss_t[s][:].rearrange("p m (g w) -> p m g w", g=GROUPS),
+                out=loss[:, tiles, GROUPS * s : GROUPS * (s + 1)],
+                in_=loss_t[s][:, tiles, :].rearrange("p m (g w) -> p m g w", g=GROUPS),
                 axis=AXIS.X,
                 op=ALU.add,
             )
             if (s + 1) % STORE == 0:
                 done = slice(GROUPS * (s + 1 - STORE), GROUPS * (s + 1))
-                nc.vector.tensor_scalar_add(loss[:, :, done], loss[:, :, done], LOST)
-                nc.sync.dma_start(out=out_v[:, :, done], in_=loss[:, :, done])
+                nc.vector.tensor_scalar_add(loss[:, tiles, done], loss[:, tiles, done], LOST)
+                nc.sync.dma_start(out=out_v[:, tiles, done], in_=loss[:, tiles, done])
 
         def step(t):
             s, h = divmod(t, 2)
@@ -398,33 +415,67 @@ def tile_decoder_kernel(
             if s >= 2 and h == 0:
                 row_sums(s - 2)
 
+        def ahead_words(s):
+            c, k = divmod(s, CHUNK)
+            if (s + SPLIT_LEAD) % CHUNK == 0 and s + SPLIT_LEAD < SLABS:
+                split_words((s + SPLIT_LEAD) // CHUNK)
+            if (s + PLACE_LEAD) % STRETCH == 0 and 2 * STRETCH <= s + PLACE_LEAD < SLABS:
+                place_scales((s + PLACE_LEAD) // STRETCH, 0, STRETCH)
+
         for j in range(PARTS):
             product_z(0, j)
-        for s in range(BATCHES[0]):
+
+        pending = []
+
+        def sig_slot(s, first_of_phase, lastone):
             sigmoids(s)
-            if s >= 1:
+            ahead_words(s)
+            if not first_of_phase:
+                factors(s - 1)
+            if s % 2 == 0:
+                emit(1)
+            if not first_of_phase:
                 quads(s - 1)
-        quads(BATCHES[0] - 1)
-        transpose_image(0, 0)
+                quad(s - 1)
+            if lastone:
+                factors(s)
+                emit(1)
+                quads(s)
+                quad(s)
+
+        def emit(n):
+            while n and pending:
+                step(pending.pop(0))
+                n -= 1
+
         first = 0
+        split_words(1)
+        for s in range(BATCHES[0]):
+            sig_slot(s, s == 0, s == BATCHES[0] - 1)
+        transpose_image(0, 0)
         for n, size in enumerate(BATCHES):
-            ahead = BATCHES[n + 1] if n + 1 < len(BATCHES) else 0
-            slots = size + ahead
-            done = 0
-            for q in range(slots):
-                if q < size:
-                    logs(first + q)
-                else:
-                    sigmoids(first + q)
-                    if q > size:
-                        quads(first + q - 1)
-                while done < (q + 1) * 2 * size // slots:
-                    step(2 * first + done)
-                    done += 1
-            if ahead:
-                quads(first + slots - 1)
+            for q in range(size):
+                s = first + q
+                logs(s)
+                if s < SLABS - 1:
+                    pending.extend([2 * s, 2 * s + 1])
+                if q:
+                    emit(2)
             first += size
-        row_sums(SLABS - 2)
+            if n + 1 < len(BATCHES):
+                for q in range(BATCHES[n + 1]):
+                    sig_slot(first + q, q == 0, q == BATCHES[n + 1] - 1)
+        emit(100)
+        last = SLABS - 1
+        transpose_image(last, 1)
         for h in range(2):
-            transpose_loss(SLABS - 1, h)
-        row_sums(SLABS - 1)
+            products(last, h, TOKEN_HALVES[0])
+        row_sums(last - 2)
+        for h in range(2):
+            transpose_loss(last - 1, h)
+        for h in range(2):
+            products(last, h, TOKEN_HALVES[1])
+        row_sums(last - 1)
+        for h in range(2):
+            transpose_loss(last, h)
+            row_sums(last, slice(2 * h, 2 * h + 2))

@@ -28,16 +28,18 @@ PARTS = 4
 SLAB = PARTS * P
 SLABS = FEATURES // SLAB
 GROUPS = SLAB // ROW
-BATCHES = (10, 11, 3)
-LIVE = 14
-CHUNK = 2
+BATCHES = (11, 10, 3)
+LIVE = 13
+CHUNK = 1
 CHUNKS = SLABS // CHUNK
-RAW_RING = 3
-WORDS_RING = 3
-IMAGE_RING = 3
+RAW_RING = 4
+WORDS_RING = 4
+IMAGE_RING = 4
 STRETCHES = P // SCALE_ROWS
 STRETCH = SLABS // STRETCHES
 STORE = 4
+STEPS_PER_LOG = (9, 5)
+STEPS_PER_SIGMOID = (2, 3)
 SPLIT_LEAD = 3
 PLACE_LEAD = 5
 Z_BANKS = 4
@@ -71,8 +73,7 @@ def tile_decoder_kernel(
         stack.enter_context(tc.manual_schedule())
         keep = stack.enter_context(tc.tile_pool(name="keep", bufs=1))
         x_pool = stack.enter_context(tc.tile_pool(name="x_pool", bufs=LIVE))
-        y_pool = stack.enter_context(tc.tile_pool(name="y_pool", bufs=LIVE))
-        pair_pool = stack.enter_context(tc.tile_pool(name="pair_pool", bufs=2))
+        pair_pool = stack.enter_context(tc.tile_pool(name="pair_pool", bufs=LIVE))
         raw_pool = stack.enter_context(tc.tile_pool(name="raw_pool", bufs=RAW_RING))
         words_pool = stack.enter_context(tc.tile_pool(name="words_pool", bufs=WORDS_RING))
         image_pool = stack.enter_context(tc.tile_pool(name="image_pool", bufs=IMAGE_RING))
@@ -103,6 +104,7 @@ def tile_decoder_kernel(
         identity_f32 = keep.tile([P, P], F32)
         ones = keep.tile([P, P], BF16)
         warm = keep.tile([P, 1], F32)
+        held = keep.tile([P, 1], F32)
         loss = keep.tile([P, TOKEN_TILES, OUTPUTS], F32)
 
         nc.vector.memset(bh_rows[:], 0.0)
@@ -173,9 +175,8 @@ def tile_decoder_kernel(
                     in_=split[first : first + 4, source].bitcast(I32),
                 )
 
-        load_words(0)
-        load_words(1)
-        load_words(2)
+        for c in range(RAW_RING):
+            load_words(c)
         load_image(0)
 
         cat_ps = psum_t.tile([P, TOKENS], BF16, tag="transposed")
@@ -252,7 +253,7 @@ def tile_decoder_kernel(
             )
 
         def exponential(m):
-            e[m] = y_pool.tile([P, PACK, P], F32, tag="y", name="e")
+            e[m] = pair_pool.tile([P, PACK, P], F32, tag="pairs", name="e")
             nc.scalar.activation(
                 out=e[m][:], in_=u[m][:], func=FUNC.Exp, scale=1.0 / SELU_SCALE, bias=math.log(SELU_SCALE * SELU_ALPHA)
             )
@@ -347,19 +348,19 @@ def tile_decoder_kernel(
 
         def quad(s):
             pairs = pair_tiles[s]
-            y = y_pool.tile([P, TOKENS], F32, tag="y")
-            nc.vector.tensor_tensor(out=y[:], in0=pairs[:, 0, :], in1=pairs[:, 1, :], op=ALU.mult)
-            y_tiles[s] = y
+            y_tiles[s] = pairs[:, 0, :]
+            nc.gpsimd.tensor_tensor(out=pairs[:, 0, :], in0=pairs[:, 0, :], in1=pairs[:, 1, :], op=ALU.mult)
 
-        def logs(s):
-            x = x_tiles[s]
+        def hold(s):
+            nc.gpsimd.tensor_copy(out=held[:], in_=x_tiles[s][:, PARTS - 1, TOKENS - 1 : TOKENS])
+
+        def log_odds(s, parts=slice(0, PARTS), tokens=slice(0, TOKENS)):
+            x = x_tiles[s][:, parts, tokens]
+            nc.scalar.activation(out=x, in_=x, func=FUNC.Ln, scale=ODDS, bias=D)
+
+        def log_quad(s):
             y = y_tiles[s]
-            if s < SLABS - 1:
-                nc.scalar.activation(out=x[:], in_=x[:], func=FUNC.Ln, scale=ODDS, bias=D)
-            nc.scalar.activation(out=y[:], in_=y[:], func=FUNC.Ln, scale=A_SCALE * A_SCALE)
-            if s == SLABS - 1:
-                for half in TOKEN_HALVES:
-                    nc.scalar.activation(out=x[:, :, half], in_=x[:, :, half], func=FUNC.Ln, scale=ODDS, bias=D)
+            nc.scalar.activation(out=y, in_=y, func=FUNC.Ln, scale=A_SCALE * A_SCALE)
 
         def transpose_image(s, h):
             c, k = divmod(s, CHUNK)
@@ -425,6 +426,9 @@ def tile_decoder_kernel(
         for j in range(PARTS):
             product_z(0, j)
 
+        def share(i, ratio):
+            return ratio[0] * (i + 1) // ratio[1] - ratio[0] * i // ratio[1]
+
         pending = []
 
         def sig_slot(s, first_of_phase, lastone):
@@ -432,16 +436,13 @@ def tile_decoder_kernel(
             ahead_words(s)
             if not first_of_phase:
                 factors(s - 1)
-            if s % 2 == 0:
-                emit(1)
+            emit(share(s, STEPS_PER_SIGMOID))
             if not first_of_phase:
                 quads(s - 1)
-                quad(s - 1)
             if lastone:
                 factors(s)
                 emit(1)
                 quads(s)
-                quad(s)
 
         def emit(n):
             while n and pending:
@@ -449,18 +450,34 @@ def tile_decoder_kernel(
                 n -= 1
 
         first = 0
-        split_words(1)
+        for c in range(1, SPLIT_LEAD):
+            split_words(c)
         for s in range(BATCHES[0]):
             sig_slot(s, s == 0, s == BATCHES[0] - 1)
         transpose_image(0, 0)
         for n, size in enumerate(BATCHES):
             for q in range(size):
                 s = first + q
-                logs(s)
+                if q == 0:
+                    quad(s)
+                if s < SLABS - 1:
+                    if q:
+                        log_odds(s)
+                    else:
+                        log_odds(s, slice(0, 2))
+                        log_odds(s, slice(2, 4))
+                    if q + 1 < size:
+                        hold(max(s - 1, first))
+                        quad(s + 1)
+                    log_quad(s)
+                else:
+                    log_quad(s)
+                    for half in TOKEN_HALVES:
+                        log_odds(s, tokens=half)
                 if s < SLABS - 1:
                     pending.extend([2 * s, 2 * s + 1])
                 if q:
-                    emit(2)
+                    emit(share(q, STEPS_PER_LOG))
             first += size
             if n + 1 < len(BATCHES):
                 for q in range(BATCHES[n + 1]):

@@ -110,10 +110,10 @@ def tile_decoder_kernel(
         nc.vector.memset(bh_rows[:], 0.0)
         nc.vector.memset(b2_rows[:], 0.0)
         nc.vector.memset(w1_raw_plane[:].bitcast(I32), 0)
-        nc.vector.memset(w2_plane[:].rearrange("p s j i -> p (s j i)").bitcast(I32), 0)
         make_identity(nc, identity[:])
         make_identity(nc, identity_f32[:])
         nc.gpsimd.memset(ones[:], 1.0)
+        nc.gpsimd.memset(w2_plane[:].rearrange("p s j i -> p (s j i)").bitcast(I32), 0)
 
         nc.sync.dma_start(out=cat[:, :, 0:32], in_=digits_v)
         nc.sync.dma_start(out=cat[:, :, 32:P], in_=styles_v)
@@ -278,25 +278,29 @@ def tile_decoder_kernel(
                 in_=grouped[m][:].rearrange("p t j -> p (t j)"),
             )
 
-        stages = [relu, bottleneck_matmul, add_b1, exponential, clamp, selu, quantise_t]
+        stages = [
+            hidden_matmuls, relu, bottleneck_matmul, add_b1, exponential, clamp, selu, quantise_t,
+        ]
 
-        def first_scales():
-            split_scales(0)
-            split_scales(1)
-            place_scales(0, 0, 2)
+        def first_scales(k):
+            split_scales(k)
+            place_scales(0, k, 1)
 
-        between = {3: prepare_b2, 4: first_scales, 5: lambda: split_words(0)}
-        for m in range(TOKEN_TILES):
-            hidden_matmuls(m)
-        prepare_w1()
         for tick in range(TOKEN_TILES + len(stages) - 1):
             for depth in reversed(range(len(stages))):
                 if 0 <= tick - depth < TOKEN_TILES:
                     stages[depth](tick - depth)
-            if tick in between:
-                between[tick]()
-        split_scales(2)
-        place_scales(0, 2, 1)
+            if tick == 1:
+                prepare_w1()
+            if tick == 7:
+                prepare_b2()
+            if tick == 6:
+                first_scales(0)
+            if tick == 8:
+                split_words(0)
+            if tick == 9:
+                first_scales(1)
+        first_scales(2)
         place_scales(1, 0, STRETCH)
         for c in range(1, IMAGE_RING):
             load_image(c)
@@ -378,8 +382,8 @@ def tile_decoder_kernel(
                 load_image(c + IMAGE_RING)
 
         def products(s, h, tokens=slice(0, TOKENS)):
-            x = x_tiles[s][:, 2 * h : 2 * h + 2, tokens]
-            img = image_t[s, h][:].bitcast(BF16).rearrange("p (t e) -> p e t", e=2)[:, :, tokens]
+            x = x_tiles[s][:, 2 * h : 2 * h + 2, tokens].rearrange("p e t -> p t e")
+            img = image_t[s, h][:].bitcast(BF16).rearrange("p (t e) -> p t e", e=2)[:, tokens, :]
             nc.vector.scalar_tensor_tensor(out=x, in0=img, scalar=-1.0, in1=x, op0=ALU.mult, op1=ALU.mult)
 
         def transpose_loss(s, h):

@@ -29,11 +29,13 @@ SLAB = PARTS * P
 SLABS = FEATURES // SLAB
 GROUPS = SLAB // ROW
 BATCHES = (11, 10, 3)
+DIRECT = (23,)
 LIVE = 13
 CHUNK = 1
+WORD_CHUNK = 2
 CHUNKS = SLABS // CHUNK
-RAW_RING = 4
-WORDS_RING = 4
+RAW_RING = 3
+WORDS_RING = 3
 IMAGE_RING = 4
 STRETCHES = P // SCALE_ROWS
 STRETCH = SLABS // STRETCHES
@@ -137,7 +139,7 @@ def tile_decoder_kernel(
         image_chunks = {}
 
         def load_words(c):
-            width = CHUNK * SLAB
+            width = WORD_CHUNK * SLAB
             raw = raw_pool.tile([P, width], I32)
             nc.sync.dma_start(out=raw[:], in_=w2_bytes.bitcast(I32)[:, c * width : (c + 1) * width])
             raw_chunks[c] = raw
@@ -148,13 +150,13 @@ def tile_decoder_kernel(
             image_chunks[c] = img
 
         def split_words(c):
-            words = words_pool.tile([P, CHUNK, PARTS, P], U32, align_bytes=64)
+            words = words_pool.tile([P, WORD_CHUNK, PARTS, P], U32, align_bytes=64)
             nc.vector.tensor_copy(
                 out=words[:].bitcast(I32).rearrange("p s j i -> p s i j"),
                 in_=raw_chunks[c][:].rearrange("p (s i j) -> p s i j", j=PARTS, i=P),
             )
             w2_chunks[c] = words
-            if c + RAW_RING < CHUNKS:
+            if c + RAW_RING < SLABS // WORD_CHUNK:
                 load_words(c + RAW_RING)
 
         def split_scales(k):
@@ -259,16 +261,15 @@ def tile_decoder_kernel(
             )
 
         def clamp(m):
-            nc.vector.tensor_scalar(
-                out=e[m][:], in0=e[m][:], scalar1=SELU_SCALE * SELU_ALPHA, scalar2=-SELU_SCALE * SELU_ALPHA,
-                op0=ALU.min, op1=ALU.add,
+            nc.scalar.activation(
+                out=e[m][:], in_=e[m][:], func=FUNC.Relu, scale=-1.0, bias=SELU_SCALE * SELU_ALPHA
             )
 
         def selu(m):
             grouped[m] = grouped_tile()
             nc.vector.scalar_tensor_tensor(
                 out=grouped[m][:], in0=u[m][:].rearrange("p j t -> p t j"), scalar=0.0,
-                in1=e[m][:].rearrange("p j t -> p t j"), op0=ALU.max, op1=ALU.add,
+                in1=e[m][:].rearrange("p j t -> p t j"), op0=ALU.max, op1=ALU.subtract,
             )
 
         def quantise_t(m):
@@ -314,7 +315,7 @@ def tile_decoder_kernel(
         pair_tiles = {}
 
         def product_z(s, j):
-            c, k = divmod(s, CHUNK)
+            c, k = divmod(s, WORD_CHUNK)
             z = psum_z.tile([P, TOKENS], F32, tag="z")
             nc.tensor.matmul_mx(
                 out=z[:],
@@ -338,6 +339,8 @@ def tile_decoder_kernel(
             x_tiles[s] = x
 
         def factors(s):
+            if s in DIRECT:
+                return
             pairs = pair_pool.tile([P, PARTS // 2, TOKENS], F32, tag="pairs")
             nc.vector.tensor_scalar(
                 out=pairs[:], in0=x_tiles[s][:, 1::2, :], scalar1=1.0, scalar2=A_SHIFT, op0=ALU.mult, op1=ALU.add
@@ -345,14 +348,18 @@ def tile_decoder_kernel(
             pair_tiles[s] = pairs
 
         def quads(s):
+            if s in DIRECT:
+                return
             pairs = pair_tiles[s]
             nc.vector.scalar_tensor_tensor(
                 out=pairs[:], in0=x_tiles[s][:, 0::2, :], scalar=A_SHIFT, in1=pairs[:], op0=ALU.add, op1=ALU.mult
             )
 
         def quad(s):
+            if s in DIRECT:
+                return
             pairs = pair_tiles[s]
-            y_tiles[s] = pairs[:, 0, :]
+            y_tiles[s] = [pairs[:, 0, :]]
             nc.gpsimd.tensor_tensor(out=pairs[:, 0, :], in0=pairs[:, 0, :], in1=pairs[:, 1, :], op=ALU.mult)
 
         def hold(s):
@@ -363,7 +370,17 @@ def tile_decoder_kernel(
             nc.scalar.activation(out=x, in_=x, func=FUNC.Ln, scale=ODDS, bias=D)
 
         def log_quad(s):
-            y = y_tiles[s]
+            if s in DIRECT:
+                y_tiles[s] = []
+                for j in (0, 2):
+                    pairs = pair_pool.tile([P, PARTS // 2, TOKENS], F32, tag="pairs", name="pairs")
+                    nc.scalar.activation(
+                        out=pairs[:], in_=x_tiles[s][:, j : j + 2, :], func=FUNC.Ln,
+                        scale=math.sqrt(A_SCALE), bias=A_SHIFT * math.sqrt(A_SCALE),
+                    )
+                    y_tiles[s].extend([pairs[:, 0, :], pairs[:, 1, :]])
+                return
+            y = y_tiles[s][0]
             nc.scalar.activation(out=y, in_=y, func=FUNC.Ln, scale=A_SCALE * A_SCALE)
 
         def transpose_image(s, h):
@@ -391,7 +408,7 @@ def tile_decoder_kernel(
                 loss_t[s] = psum_back.tile([P, TOKEN_TILES, P], F32, tag="back", name="back")
             for m in (2 * h, 2 * h + 1):
                 tokens = slice(m * P, (m + 1) * P)
-                terms = [y_tiles[s][:, tokens]] + [x_tiles[s][:, j, tokens] for j in range(PARTS)]
+                terms = [y[:, tokens] for y in y_tiles[s]] + [x_tiles[s][:, j, tokens] for j in range(PARTS)]
                 for i, term in enumerate(terms):
                     nc.tensor.matmul(
                         out=loss_t[s][:, m, :], lhsT=term, rhs=identity_f32[:],
@@ -421,9 +438,8 @@ def tile_decoder_kernel(
                 row_sums(s - 2)
 
         def ahead_words(s):
-            c, k = divmod(s, CHUNK)
-            if (s + SPLIT_LEAD) % CHUNK == 0 and s + SPLIT_LEAD < SLABS:
-                split_words((s + SPLIT_LEAD) // CHUNK)
+            if (s + SPLIT_LEAD) % WORD_CHUNK == 0 and s + SPLIT_LEAD < SLABS:
+                split_words((s + SPLIT_LEAD) // WORD_CHUNK)
             if (s + PLACE_LEAD) % STRETCH == 0 and 2 * STRETCH <= s + PLACE_LEAD < SLABS:
                 place_scales((s + PLACE_LEAD) // STRETCH, 0, STRETCH)
 
@@ -454,8 +470,7 @@ def tile_decoder_kernel(
                 n -= 1
 
         first = 0
-        for c in range(1, SPLIT_LEAD):
-            split_words(c)
+        split_words(1)
         for s in range(BATCHES[0]):
             sig_slot(s, s == 0, s == BATCHES[0] - 1)
         transpose_image(0, 0)
@@ -464,13 +479,16 @@ def tile_decoder_kernel(
                 s = first + q
                 if q == 0:
                     quad(s)
-                if s < SLABS - 1:
+                if s in DIRECT and s < SLABS - 1:
+                    log_quad(s)
+                    log_odds(s)
+                elif s < SLABS - 1:
                     if q:
                         log_odds(s)
                     else:
                         log_odds(s, slice(0, 2))
                         log_odds(s, slice(2, 4))
-                    if q + 1 < size:
+                    if q + 1 < size and s + 1 not in DIRECT:
                         hold(max(s - 1, first))
                         quad(s + 1)
                     log_quad(s)

@@ -28,8 +28,7 @@ PARTS = 4
 SLAB = PARTS * P
 SLABS = FEATURES // SLAB
 GROUPS = SLAB // ROW
-BATCHES = (11, 10, 3)
-DIRECT = (23,)
+BATCHES = (12, 12)
 LIVE = 13
 CHUNK = 1
 WORD_CHUNK = 2
@@ -40,8 +39,8 @@ IMAGE_RING = 4
 STRETCHES = P // SCALE_ROWS
 STRETCH = SLABS // STRETCHES
 STORE = 4
-STEPS_PER_LOG = (9, 5)
-STEPS_PER_SIGMOID = (2, 3)
+STEPS_PER_LOG = (19, 10)
+STEPS_PER_SIGMOID = (1, 2)
 SPLIT_LEAD = 3
 PLACE_LEAD = 5
 Z_BANKS = 4
@@ -339,8 +338,6 @@ def tile_decoder_kernel(
             x_tiles[s] = x
 
         def factors(s):
-            if s in DIRECT:
-                return
             pairs = pair_pool.tile([P, PARTS // 2, TOKENS], F32, tag="pairs")
             nc.vector.tensor_scalar(
                 out=pairs[:], in0=x_tiles[s][:, 1::2, :], scalar1=1.0, scalar2=A_SHIFT, op0=ALU.mult, op1=ALU.add
@@ -348,39 +345,25 @@ def tile_decoder_kernel(
             pair_tiles[s] = pairs
 
         def quads(s):
-            if s in DIRECT:
-                return
             pairs = pair_tiles[s]
             nc.vector.scalar_tensor_tensor(
                 out=pairs[:], in0=x_tiles[s][:, 0::2, :], scalar=A_SHIFT, in1=pairs[:], op0=ALU.add, op1=ALU.mult
             )
 
         def quad(s):
-            if s in DIRECT:
-                return
             pairs = pair_tiles[s]
-            y_tiles[s] = [pairs[:, 0, :]]
+            y_tiles[s] = pairs[:, 0, :]
             nc.gpsimd.tensor_tensor(out=pairs[:, 0, :], in0=pairs[:, 0, :], in1=pairs[:, 1, :], op=ALU.mult)
 
         def hold(s):
-            nc.gpsimd.tensor_copy(out=held[:], in_=x_tiles[s][:, PARTS - 1, TOKENS - 1 : TOKENS])
+            nc.gpsimd.tensor_copy(out=held[:], in_=y_tiles[s][:, TOKENS - 1 : TOKENS])
 
         def log_odds(s, parts=slice(0, PARTS), tokens=slice(0, TOKENS)):
             x = x_tiles[s][:, parts, tokens]
             nc.scalar.activation(out=x, in_=x, func=FUNC.Ln, scale=ODDS, bias=D)
 
         def log_quad(s):
-            if s in DIRECT:
-                y_tiles[s] = []
-                for j in (0, 2):
-                    pairs = pair_pool.tile([P, PARTS // 2, TOKENS], F32, tag="pairs", name="pairs")
-                    nc.scalar.activation(
-                        out=pairs[:], in_=x_tiles[s][:, j : j + 2, :], func=FUNC.Ln,
-                        scale=math.sqrt(A_SCALE), bias=A_SHIFT * math.sqrt(A_SCALE),
-                    )
-                    y_tiles[s].extend([pairs[:, 0, :], pairs[:, 1, :]])
-                return
-            y = y_tiles[s][0]
+            y = y_tiles[s]
             nc.scalar.activation(out=y, in_=y, func=FUNC.Ln, scale=A_SCALE * A_SCALE)
 
         def transpose_image(s, h):
@@ -408,7 +391,7 @@ def tile_decoder_kernel(
                 loss_t[s] = psum_back.tile([P, TOKEN_TILES, P], F32, tag="back", name="back")
             for m in (2 * h, 2 * h + 1):
                 tokens = slice(m * P, (m + 1) * P)
-                terms = [y[:, tokens] for y in y_tiles[s]] + [x_tiles[s][:, j, tokens] for j in range(PARTS)]
+                terms = [y_tiles[s][:, tokens]] + [x_tiles[s][:, j, tokens] for j in range(PARTS)]
                 for i, term in enumerate(terms):
                     nc.tensor.matmul(
                         out=loss_t[s][:, m, :], lhsT=term, rhs=identity_f32[:],
@@ -424,7 +407,10 @@ def tile_decoder_kernel(
             )
             if (s + 1) % STORE == 0:
                 done = slice(GROUPS * (s + 1 - STORE), GROUPS * (s + 1))
-                nc.vector.tensor_scalar_add(loss[:, tiles, done], loss[:, tiles, done], LOST)
+                engine = nc.vector if s + 1 == SLABS else nc.gpsimd
+                engine.tensor_scalar(
+                    out=loss[:, tiles, done], in0=loss[:, tiles, done], scalar1=1.0, scalar2=LOST, op0=ALU.mult, op1=ALU.add
+                )
                 nc.sync.dma_start(out=out_v[:, tiles, done], in_=loss[:, tiles, done])
 
         def step(t):
@@ -479,17 +465,15 @@ def tile_decoder_kernel(
                 s = first + q
                 if q == 0:
                     quad(s)
-                if s in DIRECT and s < SLABS - 1:
-                    log_quad(s)
-                    log_odds(s)
-                elif s < SLABS - 1:
+                    quad(s + 1)
+                if s < SLABS - 1:
                     if q:
                         log_odds(s)
                     else:
                         log_odds(s, slice(0, 2))
                         log_odds(s, slice(2, 4))
-                    if q + 1 < size and s + 1 not in DIRECT:
-                        hold(max(s - 1, first))
+                    if q and q + 1 < size:
+                        hold(s - 1)
                         quad(s + 1)
                     log_quad(s)
                 else:

from contextlib import ExitStack
import math

import concourse.mybir as mybir
from concourse.masks import make_identity

F32 = mybir.dt.float32
BF16 = mybir.dt.bfloat16
U8 = mybir.dt.uint8
U32 = mybir.dt.uint32
I32 = mybir.dt.int32
FP8X4 = mybir.dt.float8_e4m3fn_x4
ALU = mybir.AluOpType
FUNC = mybir.ActivationFunctionType
AXIS = mybir.AxisListType

P = 128
SCALE_ROWS = 16
PACK = 4
TOKENS = 512
TOKEN_TILES = TOKENS // P
TOKEN_HALVES = (slice(0, TOKENS // 2), slice(TOKENS // 2, TOKENS))
HIDDEN = 512
FEATURES = 12288
ROW = 64
OUTPUTS = FEATURES // ROW
PARTS = 4
SLAB = PARTS * P
SLABS = FEATURES // SLAB
GROUPS = SLAB // ROW
BATCHES = (12, 12)
LIVE = 13
CHUNK = 1
WORD_CHUNK = 2
CHUNKS = SLABS // CHUNK
RAW_RING = 3
WORDS_RING = 3
IMAGE_RING = 4
STRETCHES = P // SCALE_ROWS
STRETCH = SLABS // STRETCHES
STORE = 4
STEPS_PER_LOG = (19, 10)
STEPS_PER_SIGMOID = (1, 2)
SPLIT_LEAD = 3
PLACE_LEAD = 5
Z_BANKS = 4

EPS = 1e-9
D = EPS / (1.0 + EPS)
ODDS = 1.0 / D - D
A_SCALE = ODDS / (1.0 + 2.0 * EPS)
A_SHIFT = (1.0 + D) / ODDS
QUADS = ROW // PARTS
LOST = QUADS * 2.0 * math.log(A_SCALE)
SELU_ALPHA = 1.6732632423543772848170429916717
SELU_SCALE = 1.0507009873554804934193349852946

FLOPS = 2 * TOKENS * (P * HIDDEN + HIDDEN * HIDDEN + HIDDEN * FEATURES)


def tile_decoder_kernel(
    tc, digits, styles, images, W_h, b_h, W1_words, W1_scales, b1, W2_words, W2_scales, b2, out
):
    nc = tc.nc

    digits_v = digits.rearrange("s b d -> (s b) d").rearrange("(m p) d -> p m d", p=P)
    styles_v = styles.rearrange("s b d -> (s b) d").rearrange("(m p) d -> p m d", p=P)
    images_v = images.rearrange("s b c h w -> (s b) (c h w)").rearrange("(m p) f -> p m f", p=P)
    out_v = out.rearrange("s b c h -> (s b) (c h)").rearrange("(m p) g -> p m g", p=P)
    w1_bytes = W1_words[0].rearrange("p n t -> p (n t)")
    w2_bytes = W2_words[0].rearrange("p n t -> p (n t)")

    with ExitStack() as stack:
        stack.enter_context(tc.manual_schedule())
        keep = stack.enter_context(tc.tile_pool(name="keep", bufs=1))
        x_pool = stack.enter_context(tc.tile_pool(name="x_pool", bufs=LIVE))
        pair_pool = stack.enter_context(tc.tile_pool(name="pair_pool", bufs=LIVE))
        raw_pool = stack.enter_context(tc.tile_pool(name="raw_pool", bufs=RAW_RING))
        words_pool = stack.enter_context(tc.tile_pool(name="words_pool", bufs=WORDS_RING))
        image_pool = stack.enter_context(tc.tile_pool(name="image_pool", bufs=IMAGE_RING))
        psum_z = stack.enter_context(tc.psum_pool(name="psum_z", bufs=Z_BANKS))
        psum_t = stack.enter_context(tc.psum_pool(name="psum_t", bufs=2))
        psum_back = stack.enter_context(tc.psum_pool(name="psum_back", bufs=2))

        cat = keep.tile([P, TOKEN_TILES, P], BF16)
        cat_t = keep.tile([P, TOKENS], BF16)
        wh = keep.tile([P, HIDDEN], BF16)
        bh_rows = keep.tile([P, HIDDEN], BF16)
        b1_t = keep.tile([P, PACK], BF16)
        b1_scaled = keep.tile([P, PACK], F32)
        b2_rows = keep.tile([P, SLAB], BF16)
        b2_t = keep.tile([P, PARTS, P], F32)
        w1_raw = keep.tile([P, HIDDEN], I32)
        w1_raw_plane = keep.tile([P, HIDDEN], U8, align_bytes=64)
        w1_words = keep.tile([P, PACK, P], U32, align_bytes=64)
        w1_plane = keep.tile([P, PACK, P], U8, align_bytes=64)
        w2_scales = keep.tile([P, STRETCH * SLAB], U8, align_bytes=64)
        w2_split_scales = keep.tile([P, STRETCH, PARTS, P], U8, align_bytes=64)
        w2_plane = keep.tile([P, SLABS, PARTS, P], U8, align_bytes=64)
        h_words = keep.tile([P, TOKEN_TILES, P], U32, align_bytes=64)
        h_plane = keep.tile([P, TOKEN_TILES, P], U8, align_bytes=64)
        t_words = keep.tile([P, TOKENS], U32, align_bytes=64)
        t_plane = keep.tile([P, TOKENS], U8, align_bytes=64)
        identity = keep.tile([P, P], BF16)
        identity_f32 = keep.tile([P, P], F32)
        ones = keep.tile([P, P], BF16)
        warm = keep.tile([P, 1], F32)
        held = keep.tile([P, 1], F32)
        loss = keep.tile([P, TOKEN_TILES, OUTPUTS], F32)

        nc.vector.memset(bh_rows[:], 0.0)
        nc.vector.memset(b2_rows[:], 0.0)
        nc.vector.memset(w1_raw_plane[:].bitcast(I32), 0)
        make_identity(nc, identity[:])
        make_identity(nc, identity_f32[:])
        nc.gpsimd.memset(ones[:], 1.0)
        nc.gpsimd.memset(w2_plane[:].rearrange("p s j i -> p (s j i)").bitcast(I32), 0)

        nc.sync.dma_start(out=cat[:, :, 0:32], in_=digits_v)
        nc.sync.dma_start(out=cat[:, :, 32:P], in_=styles_v)
        nc.sync.dma_start(out=wh[:], in_=W_h)
        nc.sync.dma_start(out=bh_rows[0:1, :], in_=b_h.rearrange("(o n) -> o n", o=1))
        nc.sync.dma_start(out=w1_raw[:], in_=w1_bytes.bitcast(I32))
        nc.sync.dma_start(out=b1_t[:], in_=b1.rearrange("(p j) -> p j", j=PACK))
        nc.sync.dma_start(out=b2_rows[0:SLABS, :], in_=b2.rearrange("(s f) -> s f", f=SLAB))
        for quadrant in range(4):
            rows = slice(4 * quadrant, 4 * quadrant + 4)
            live = slice(32 * quadrant, 32 * quadrant + 4)
            nc.sync.dma_start(out=w1_raw_plane[live, :].bitcast(I32), in_=W1_scales[0, rows, :].bitcast(I32))
        for b in range(STRETCHES):
            nc.sync.dma_start(
                out=w2_scales[b * SCALE_ROWS : (b + 1) * SCALE_ROWS, :].bitcast(I32),
                in_=W2_scales[0, :, b * STRETCH * SLAB : (b + 1) * STRETCH * SLAB].bitcast(I32),
            )

        raw_chunks = {}
        w2_chunks = {}
        image_chunks = {}

        def load_words(c):
            width = WORD_CHUNK * SLAB
            raw = raw_pool.tile([P, width], I32)
            nc.sync.dma_start(out=raw[:], in_=w2_bytes.bitcast(I32)[:, c * width : (c + 1) * width])
            raw_chunks[c] = raw

        def load_image(c):
            img = image_pool.tile([P, TOKEN_TILES, CHUNK * SLAB], BF16)
            nc.sync.dma_start(out=img[:], in_=images_v[:, :, c * CHUNK * SLAB : (c + 1) * CHUNK * SLAB])
            image_chunks[c] = img

        def split_words(c):
            words = words_pool.tile([P, WORD_CHUNK, PARTS, P], U32, align_bytes=64)
            nc.vector.tensor_copy(
                out=words[:].bitcast(I32).rearrange("p s j i -> p s i j"),
                in_=raw_chunks[c][:].rearrange("p (s i j) -> p s i j", j=PARTS, i=P),
            )
            w2_chunks[c] = words
            if c + RAW_RING < SLABS // WORD_CHUNK:
                load_words(c + RAW_RING)

        def split_scales(k):
            nc.vector.tensor_copy(
                out=w2_split_scales[:, k, :, :].rearrange("p j i -> p i j"),
                in_=w2_scales[:, k * SLAB : (k + 1) * SLAB].rearrange("p (i j) -> p i j", j=PARTS),
            )

        def place_scales(b, k, count):
            split = w2_split_scales[:].rearrange("p s j i -> p (s j i)")
            plane = w2_plane[:].rearrange("p s j i -> p (s j i)")
            source = slice(k * SLAB, (k + count) * SLAB)
            target = slice((b * STRETCH + k) * SLAB, (b * STRETCH + k + count) * SLAB)
            for quadrant in range(4):
                first = b * SCALE_ROWS + 4 * quadrant
                nc.sync.dma_start(
                    out=plane[32 * quadrant : 32 * quadrant + 4, target].bitcast(I32),
                    in_=split[first : first + 4, source].bitcast(I32),
                )

        for c in range(RAW_RING):
            load_words(c)
        load_image(0)

        cat_ps = psum_t.tile([P, TOKENS], BF16, tag="transposed")
        for m in range(TOKEN_TILES):
            nc.tensor.transpose(cat_ps[:, m * P : (m + 1) * P], cat[:, m, :], identity[:])
        nc.vector.tensor_copy(out=cat_t[:], in_=cat_ps[:])
        wh_v = wh[:].rearrange("k (p j) -> k j p", j=PACK)
        bh_v = bh_rows[:].rearrange("k (p j) -> k j p", j=PACK)

        h_ps = {}
        t_ps = {}
        u = {}
        e = {}
        grouped = {}

        def grouped_tile():
            return keep.tile([P, P, PACK], BF16, tag="grouped", bufs=TOKEN_TILES, align_bytes=64, name="grouped")

        def prepare_w1():
            nc.vector.tensor_copy(
                out=w1_words[:].bitcast(I32).rearrange("k j p -> k p j"), in_=w1_raw[:].rearrange("k (p j) -> k p j", j=PACK)
            )
            nc.vector.tensor_copy(
                out=w1_plane[:].rearrange("k j p -> k p j"), in_=w1_raw_plane[:].rearrange("k (p j) -> k p j", j=PACK)
            )
            nc.vector.tensor_scalar_mul(b1_scaled[:], b1_t[:], SELU_SCALE)

        def prepare_b2():
            b2_ps = psum_t.tile([P, PARTS, P], BF16, tag="transposed")
            for j in range(PARTS):
                nc.tensor.transpose(b2_ps[:, j, :], b2_rows[:, j::PARTS], identity[:])
            nc.scalar.activation(out=b2_t[:], in_=b2_ps[:], func=FUNC.Identity, bias=math.log(D))

        def hidden_matmuls(m):
            h_ps[m] = psum_z.tile([P, PACK, P], F32, tag="z", name="h_ps")
            for j in range(PACK):
                nc.tensor.matmul(
                    out=h_ps[m][:, j, :], lhsT=wh_v[:, j, :], rhs=cat_t[:, m * P : (m + 1) * P],
                    start=True, stop=False,
                )
                nc.tensor.matmul(
                    out=h_ps[m][:, j, :], lhsT=bh_v[:, j, :], rhs=ones[:], start=False, stop=True
                )

        def relu(m):
            grouped[m] = grouped_tile()
            nc.scalar.activation(
                out=grouped[m][:], in_=h_ps[m][:].rearrange("p j t -> p t j"), func=FUNC.Relu
            )

        def bottleneck_matmul(m):
            nc.vector.quantize_mx(
                out=h_words[:, m, :].bitcast(FP8X4),
                scales=h_plane[:, m, :],
                in_=grouped[m][:].rearrange("p t j -> p (t j)"),
            )
            t_ps[m] = psum_z.tile([P, PACK, P], F32, tag="z", name="t_ps")
            for j in range(PACK):
                nc.tensor.matmul_mx(
                    out=t_ps[m][:, j, :],
                    lhsT=w1_words[:, j, :].bitcast(FP8X4),
                    lhsT_scale=w1_plane[:, j, :],
                    rhs=h_words[:, m, :].bitcast(FP8X4),
                    rhs_scale=h_plane[:, m, :],
                    start=True,
                    stop=True,
                )

        def add_b1(m):
            u[m] = x_pool.tile([P, PACK, P], F32, tag="x", name="u")
            nc.vector.scalar_tensor_tensor(
                out=u[m][:], in0=t_ps[m][:], scalar=SELU_SCALE,
                in1=b1_scaled[:].unsqueeze(2).to_broadcast([P, PACK, P]), op0=ALU.mult, op1=ALU.add,
            )

        def exponential(m):
            e[m] = pair_pool.tile([P, PACK, P], F32, tag="pairs", name="e")
            nc.scalar.activation(
                out=e[m][:], in_=u[m][:], func=FUNC.Exp, scale=1.0 / SELU_SCALE, bias=math.log(SELU_SCALE * SELU_ALPHA)
            )

        def clamp(m):
            nc.scalar.activation(
                out=e[m][:], in_=e[m][:], func=FUNC.Relu, scale=-1.0, bias=SELU_SCALE * SELU_ALPHA
            )

        def selu(m):
            grouped[m] = grouped_tile()
            nc.vector.scalar_tensor_tensor(
                out=grouped[m][:], in0=u[m][:].rearrange("p j t -> p t j"), scalar=0.0,
                in1=e[m][:].rearrange("p j t -> p t j"), op0=ALU.max, op1=ALU.subtract,
            )

        def quantise_t(m):
            nc.vector.quantize_mx(
                out=t_words[:, m * P : (m + 1) * P].bitcast(FP8X4),
                scales=t_plane[:, m * P : (m + 1) * P],
                in_=grouped[m][:].rearrange("p t j -> p (t j)"),
            )

        stages = [
            hidden_matmuls, relu, bottleneck_matmul, add_b1, exponential, clamp, selu, quantise_t,
        ]

        def first_scales(k):
            split_scales(k)
            place_scales(0, k, 1)

        for tick in range(TOKEN_TILES + len(stages) - 1):
            for depth in reversed(range(len(stages))):
                if 0 <= tick - depth < TOKEN_TILES:
                    stages[depth](tick - depth)
            if tick == 1:
                prepare_w1()
            if tick == 7:
                prepare_b2()
            if tick == 6:
                first_scales(0)
            if tick == 8:
                split_words(0)
            if tick == 9:
                first_scales(1)
        first_scales(2)
        place_scales(1, 0, STRETCH)
        for c in range(1, IMAGE_RING):
            load_image(c)
        nc.scalar.activation(out=warm[:], in_=ones[:, 0:1], func=FUNC.Sigmoid)

        z_tiles = {}
        x_tiles = {}
        y_tiles = {}
        image_t = {}
        loss_t = {}
        pair_tiles = {}

        def product_z(s, j):
            c, k = divmod(s, WORD_CHUNK)
            z = psum_z.tile([P, TOKENS], F32, tag="z")
            nc.tensor.matmul_mx(
                out=z[:],
                lhsT=w2_chunks[c][:, k, j, :].bitcast(FP8X4),
                lhsT_scale=w2_plane[:, s, j, :],
                rhs=t_words[:].bitcast(FP8X4),
                rhs_scale=t_plane[:],
                start=True,
                stop=True,
            )
            z_tiles[s, j] = z

        def sigmoids(s):
            x = x_pool.tile([P, PARTS, TOKENS], F32, tag="x")
            for j in range(PARTS):
                nc.scalar.activation(
                    out=x[:, j, :], in_=z_tiles[s, j][:], func=FUNC.Sigmoid, bias=b2_t[:, j, s : s + 1]
                )
                if s + 1 < SLABS:
                    product_z(s + 1, j)
            x_tiles[s] = x

        def factors(s):
            pairs = pair_pool.tile([P, PARTS // 2, TOKENS], F32, tag="pairs")
            nc.vector.tensor_scalar(
                out=pairs[:], in0=x_tiles[s][:, 1::2, :], scalar1=1.0, scalar2=A_SHIFT, op0=ALU.mult, op1=ALU.add
            )
            pair_tiles[s] = pairs

        def quads(s):
            pairs = pair_tiles[s]
            nc.vector.scalar_tensor_tensor(
                out=pairs[:], in0=x_tiles[s][:, 0::2, :], scalar=A_SHIFT, in1=pairs[:], op0=ALU.add, op1=ALU.mult
            )

        def quad(s):
            pairs = pair_tiles[s]
            y_tiles[s] = pairs[:, 0, :]
            nc.gpsimd.tensor_tensor(out=pairs[:, 0, :], in0=pairs[:, 0, :], in1=pairs[:, 1, :], op=ALU.mult)

        def hold(s):
            nc.gpsimd.tensor_copy(out=held[:], in_=y_tiles[s][:, TOKENS - 1 : TOKENS])

        def log_odds(s, parts=slice(0, PARTS), tokens=slice(0, TOKENS)):
            x = x_tiles[s][:, parts, tokens]
            nc.scalar.activation(out=x, in_=x, func=FUNC.Ln, scale=ODDS, bias=D)

        def log_quad(s):
            y = y_tiles[s]
            nc.scalar.activation(out=y, in_=y, func=FUNC.Ln, scale=A_SCALE * A_SCALE)

        def transpose_image(s, h):
            c, k = divmod(s, CHUNK)
            words = image_chunks[c][:].rearrange("p m f -> p (m f)").bitcast(F32)
            words = words.rearrange("p (m f) -> p m f", m=TOKEN_TILES)
            img_t = psum_t.tile([P, TOKENS], F32, tag="transposed")
            for m in range(TOKEN_TILES):
                nc.tensor.transpose(
                    img_t[:, m * P : (m + 1) * P],
                    words[:, m, k * SLAB // 2 + h : (k + 1) * SLAB // 2 : 2],
                    identity_f32[:],
                )
            image_t[s, h] = img_t
            if h == 1 and k == CHUNK - 1 and c + IMAGE_RING < CHUNKS:
                load_image(c + IMAGE_RING)

        def products(s, h, tokens=slice(0, TOKENS)):
            x = x_tiles[s][:, 2 * h : 2 * h + 2, tokens].rearrange("p e t -> p t e")
            img = image_t[s, h][:].bitcast(BF16).rearrange("p (t e) -> p t e", e=2)[:, tokens, :]
            nc.vector.scalar_tensor_tensor(out=x, in0=img, scalar=-1.0, in1=x, op0=ALU.mult, op1=ALU.mult)

        def transpose_loss(s, h):
            if h == 0:
                loss_t[s] = psum_back.tile([P, TOKEN_TILES, P], F32, tag="back", name="back")
            for m in (2 * h, 2 * h + 1):
                tokens = slice(m * P, (m + 1) * P)
                terms = [y_tiles[s][:, tokens]] + [x_tiles[s][:, j, tokens] for j in range(PARTS)]
                for i, term in enumerate(terms):
                    nc.tensor.matmul(
                        out=loss_t[s][:, m, :], lhsT=term, rhs=identity_f32[:],
                        is_transpose=True, start=i == 0, stop=i == len(terms) - 1,
                    )

        def row_sums(s, tiles=slice(0, TOKEN_TILES)):
            nc.vector.tensor_reduce(
                out=loss[:, tiles, GROUPS * s : GROUPS * (s + 1)],
                in_=loss_t[s][:, tiles, :].rearrange("p m (g w) -> p m g w", g=GROUPS),
                axis=AXIS.X,
                op=ALU.add,
            )
            if (s + 1) % STORE == 0:
                done = slice(GROUPS * (s + 1 - STORE), GROUPS * (s + 1))
                engine = nc.vector if s + 1 == SLABS else nc.gpsimd
                engine.tensor_scalar(
                    out=loss[:, tiles, done], in0=loss[:, tiles, done], scalar1=1.0, scalar2=LOST, op0=ALU.mult, op1=ALU.add
                )
                nc.sync.dma_start(out=out_v[:, tiles, done], in_=loss[:, tiles, done])

        def step(t):
            s, h = divmod(t, 2)
            if t + 1 < 2 * SLABS:
                transpose_image(*divmod(t + 1, 2))
            products(s, h)
            if s >= 1:
                transpose_loss(s - 1, h)
            if s >= 2 and h == 0:
                row_sums(s - 2)

        def ahead_words(s):
            if (s + SPLIT_LEAD) % WORD_CHUNK == 0 and s + SPLIT_LEAD < SLABS:
                split_words((s + SPLIT_LEAD) // WORD_CHUNK)
            if (s + PLACE_LEAD) % STRETCH == 0 and 2 * STRETCH <= s + PLACE_LEAD < SLABS:
                place_scales((s + PLACE_LEAD) // STRETCH, 0, STRETCH)

        for j in range(PARTS):
            product_z(0, j)

        def share(i, ratio):
            return ratio[0] * (i + 1) // ratio[1] - ratio[0] * i // ratio[1]

        pending = []

        def sig_slot(s, first_of_phase, lastone):
            sigmoids(s)
            ahead_words(s)
            if not first_of_phase:
                factors(s - 1)
            emit(share(s, STEPS_PER_SIGMOID))
            if not first_of_phase:
                quads(s - 1)
            if lastone:
                factors(s)
                emit(1)
                quads(s)

        def emit(n):
            while n and pending:
                step(pending.pop(0))
                n -= 1

        first = 0
        split_words(1)
        for s in range(BATCHES[0]):
            sig_slot(s, s == 0, s == BATCHES[0] - 1)
        transpose_image(0, 0)
        for n, size in enumerate(BATCHES):
            for q in range(size):
                s = first + q
                if q == 0:
                    quad(s)
                    quad(s + 1)
                if s < SLABS - 1:
                    if q:
                        log_odds(s)
                    else:
                        log_odds(s, slice(0, 2))
                        log_odds(s, slice(2, 4))
                    if q and q + 1 < size:
                        hold(s - 1)
                        quad(s + 1)
                    log_quad(s)
                else:
                    log_quad(s)
                    for half in TOKEN_HALVES:
                        log_odds(s, tokens=half)
                if s < SLABS - 1:
                    pending.extend([2 * s, 2 * s + 1])
                if q:
                    emit(share(q, STEPS_PER_LOG))
            first += size
            if n + 1 < len(BATCHES):
                for q in range(BATCHES[n + 1]):
                    sig_slot(first + q, q == 0, q == BATCHES[n + 1] - 1)
        emit(100)
        last = SLABS - 1
        transpose_image(last, 1)
        for h in range(2):
            products(last, h, TOKEN_HALVES[0])
        row_sums(last - 2)
        for h in range(2):
            transpose_loss(last - 1, h)
        for h in range(2):
            products(last, h, TOKEN_HALVES[1])
        row_sums(last - 1)
        for h in range(2):
            transpose_loss(last, h)
            row_sums(last, slice(2 * h, 2 * h + 2))
